import numpy as np
import ml_dtypes


def mxq(x, axis, fmt="e4m3"):
    dtype, down = {"e4m3": (ml_dtypes.float8_e4m3fn, 7), "e5m2": (ml_dtypes.float8_e5m2, 14)}[fmt]
    v = np.moveaxis(np.asarray(x, np.float32).astype(ml_dtypes.bfloat16).astype(np.float64), axis, -1)
    blocks = v.reshape(v.shape[:-1] + (-1, 32))
    amax = np.abs(blocks).max(-1, keepdims=True)
    byte = np.maximum(np.where(amax > 0, np.frexp(amax)[1] - 1 + 127, 0) - down, 1)
    scale = np.exp2(byte - 127.0)
    codes = (blocks / scale).astype(np.float32).astype(dtype).astype(np.float64)
    return np.moveaxis((codes * scale).reshape(v.shape), -1, axis)


WIDE = False


def mx_kscale(k):
    if not WIDE:
        return np.ones(k)
    levels = np.array([10, -10, 5, -5, 0])
    if k % 512:
        return np.exp2(np.random.permutation(np.resize(levels, k // 32))).repeat(32)
    a = np.empty((k // 512, 16))
    for p in range(k // 512):
        a[p, :8] = np.random.permutation(np.resize(levels, 8))
        for g in range(8):
            far = levels[np.abs(levels - a[p, g]) >= 10]
            a[p, g + 8] = far[np.random.randint(len(far))]
    return np.exp2(a.ravel()).repeat(32)


BF16 = ml_dtypes.bfloat16


def bf(x):
    return np.asarray(x, np.float32).astype(BF16)


def f64(x):
    return np.asarray(x).astype(np.float64)


B, H, W, DIM, NH, HD, WH, WW = 8, 16, 16, 512, 16, 32, 8, 8
E = NH * HD
N = WH * WW
HALF = HD // 2


def cos_sin(n):
    inv_freq = 1.0 / (10000.0 ** (f64(np.arange(0, HALF, 2)) / HALF))
    ang = f64(np.arange(n))[:, None] * inv_freq
    return np.concatenate([np.cos(ang)] * 2, -1), np.concatenate([np.sin(ang)] * 2, -1)


def rot_half(u):
    u1, u2 = np.split(u, 2, axis=-1)
    return np.concatenate([-u2, u1], -1)


def rope2(t):
    cos_h, sin_h = cos_sin(WH)
    cos_w, sin_w = cos_sin(WW)
    th, tw = t[..., :HALF], t[..., HALF:]
    th = th * cos_h[:, None, :] + rot_half(th) * sin_h[:, None, :]
    tw = tw * cos_w[None, :, :] + rot_half(tw) * sin_w[None, :, :]
    return np.concatenate([th, tw], -1)


def draw0():
    s = mx_kscale(DIM)
    return {"x": bf(np.random.standard_normal((B, H, W, DIM)) * s),
            "qkv_w": bf(np.random.standard_normal((DIM, 3 * E)) / np.sqrt(DIM) / s[:, None]),
            "qkv_b": bf(np.random.standard_normal(3 * E) * 0.3)}


def core(x, qkv_w, qkv_b):
    xw = f64(x).reshape(B, H // WH, WH, W // WW, WW, DIM).transpose(0, 1, 3, 2, 4, 5).reshape(-1, N, DIM)
    BW = xw.shape[0]
    qkv = (mxq(xw, 2, "e4m3") @ mxq(f64(qkv_w), 0, "e4m3")) + f64(qkv_b)
    qkv = qkv.reshape(BW, N, 3, NH, HD).transpose(2, 0, 3, 1, 4)
    q, k, v = qkv[0], qkv[1], qkv[2]
    q = rope2(q.reshape(-1, WH, WW, HD)).reshape(BW, NH, N, HD)
    k = rope2(k.reshape(-1, WH, WW, HD)).reshape(BW, NH, N, HD)
    return q, k, np.ascontiguousarray(v)


def e4m3fn_bytes(y):
    return np.clip(np.asarray(y, np.float64), -448.0, 448.0).astype(np.float32).astype(ml_dtypes.float8_e4m3fn).view(np.uint8)


def e4m3fn_values(b):
    return np.asarray(b, np.uint8).view(ml_dtypes.float8_e4m3fn).astype(np.float64)


def setup_inputs():
    d = draw0()
    x0 = np.asarray(d['x']).astype(np.float64)
    s = (np.max(np.abs(x0), axis=(0, 1, 2), keepdims=True) / 448.0).astype(np.float32)
    out = {}
    for k, v in d.items():
        if k == 'x':
            out['x_bytes'] = e4m3fn_bytes(x0 / s.astype(np.float64))
            out['x_scale'] = s
        else:
            out[k] = v
    return out


def reference(x_bytes, x_scale, qkv_w, qkv_b):
    return core(e4m3fn_values(x_bytes) * x_scale.astype(np.float64), qkv_w, qkv_b)

@@ -1,0 +1,380 @@
+import math
+from contextlib import ExitStack
+
+import concourse.mybir as mybir
+from concourse.masks import make_identity
+
+FLOPS = 2 * 2048 * 512 * 1536
+
+F32 = mybir.dt.float32
+BF16 = mybir.dt.bfloat16
+U32 = mybir.dt.uint32
+U8 = mybir.dt.uint8
+FP8 = mybir.dt.float8_e4m3fn
+FP8X4 = mybir.dt.float8_e4m3fn_x4
+ALU = mybir.AluOpType
+ACTF = mybir.ActivationFunctionType
+AX = mybir.AxisListType
+
+P = 128
+NPOS = 8
+NFREQ = 8
+NH = 16
+HD = 32
+E = 512
+KDIM = 512
+CHUNK = 512
+
+UNITS = [(pq, rb, ch) for rb in range(2) for ch in range(2) for pq in range(2)]
+NPAIR = 2 * len(UNITS)
+P_B_ON_V = frozenset((11, 15))
+EV_ON_V = frozenset(((7, 1), (7, 3)))
+V_AT = {0: ((0, 0), (0, 1)), 1: ((0, 2), (0, 3)), 4: ((0, 4), (0, 5)), 5: ((0, 6), (0, 7)), 7: ((1, 0), (1, 1)), 8: ((1, 2), (1, 3)), 10: ((1, 4), (1, 5)), 11: ((1, 6), (1, 7))}
+XDEQ_AT = {0: ((1, 0),), 1: ((1, 1),), 3: ((2, 0),), 4: ((2, 1),), 6: ((3, 0),), 7: ((3, 1),)}
+MX_LEAD = 1
+V_HALF = False
+HALF_FROM = 8
+
+
+def tile_hydra_attn_pa_kernel(tc, x_bytes, x_scale, qkv_w, qkv_b, out_0, out_1, out_2):
+    nc = tc.nc
+    outs = (out_0, out_1, out_2)
+
+    with ExitStack() as ctx:
+        const = ctx.enter_context(tc.tile_pool(name="const", bufs=1))
+        xwork = ctx.enter_context(tc.tile_pool(name="xwork", bufs=3))
+        wwork = ctx.enter_context(tc.tile_pool(name="wwork", bufs=2))
+        rot = ctx.enter_context(tc.tile_pool(name="rot", bufs=3))
+        psum = ctx.enter_context(tc.psum_pool(name="psum", bufs=8))
+        ctx.enter_context(tc.manual_schedule())
+
+        sc = const.tile([P, KDIM], F32, name="sc")
+        x_rows = x_bytes.rearrange("b (wi rp rb) (j c) k -> rb (b wi rp) j (c k)", wi=2, rp=4, rb=2, j=2)
+        w_rows = qkv_w.rearrange("(p t) n -> p t n", t=4)
+        xb = []
+        wraw = []
+        for T in range(4):
+            xb_T = const.tile([P, 4 * KDIM], U8, name="xb%d" % T)
+            xb.append(xb_T)
+        for part in range(3):
+            wraw_p = const.tile([P, 4, E], BF16, name="wraw%d" % part)
+            wraw.append(wraw_p)
+
+        def load_x(T):
+            nc.sync.dma_start(out=xb[T][:], in_=x_rows[T // 2, :, :, (T % 2) * 2048:(T % 2 + 1) * 2048])
+
+        def load_w(part):
+            nc.sync.dma_start(out=wraw[part][:], in_=w_rows[:, :, part * E:(part + 1) * E])
+
+        brow = const.tile([P, P], BF16, name="brow")
+        nc.vector.memset(brow[:], 0.0)
+        load_x(0)
+        nc.sync.dma_start(out=sc[:], in_=x_scale.rearrange("a b c k -> (a b c k)").partition_broadcast(P))
+        for q in range(2):
+            nc.sync.dma_start(
+                out=brow[q * 4:(q + 1) * 4, :].rearrange("p (h i) -> p h i", i=NFREQ),
+                in_=qkv_b[q * E:(q + 1) * E].rearrange("(h f i) -> f h i", h=NH, f=4, i=NFREQ),
+            )
+        load_w(0)
+        load_w(1)
+        load_w(2)
+        bv = const.tile([P, E], BF16, name="bv")
+        nc.sync.dma_start(out=bv[:], in_=qkv_b[2 * E:3 * E].partition_broadcast(P))
+        load_x(1)
+        load_x(2)
+        load_x(3)
+
+        ident = const.tile([P, P], F32, name="ident")
+        make_identity(nc, ident[:])
+        zo = const.tile([P, 2], F32, name="zo")
+        nc.vector.memset(zo[:, 0:1], 0.0)
+        nc.vector.memset(zo[:, 1:2], 1.0)
+        tab = const.tile([P, 2, NPOS, NFREQ], F32, name="tab")
+        nc.vector.memset(tab[:, 0, 0, :], 1.0)
+        nc.vector.memset(tab[:, 1, 0, :], 0.0)
+        for pos in range(1, NPOS):
+            for s in range(2):
+                for i in range(0, NFREQ, 2):
+                    ang = (pos * 10000.0 ** (-i / 8.0), pos * 10000.0 ** (-(i + 1) / 8.0))
+                    va = math.cos(ang[0]) if s == 0 else math.sin(ang[0])
+                    vb = math.cos(ang[1]) if s == 0 else math.sin(ang[1])
+                    dst = tab[:, s, pos, i:i + 2]
+                    if s == 0:
+                        nc.vector.tensor_scalar(out=dst, in0=zo[:], scalar1=vb - va, scalar2=va, op0=ALU.mult,
+                                                op1=ALU.add)
+                    else:
+                        nc.scalar.activation(out=dst, in_=zo[:], func=ACTF.Copy, bias=va, scale=vb - va)
+        perm = const.tile([P, P], F32, name="perm")
+        nc.vector.tensor_copy(out=perm[:].rearrange("p (b j r) -> p b j r", b=16, j=2, r=4),
+                              in_=ident[:].rearrange("p (b r j) -> p b j r", b=16, r=4, j=2))
+        pick = const.tile([P, NFREQ], F32, name="pick")
+        nc.vector.tensor_reduce(out=pick[:], in_=ident[:].rearrange("p (h i) -> p i h", i=NFREQ), axis=AX.X, op=ALU.add)
+        tabm = const.tile([P, 2 * NPOS, NFREQ], F32, name="tabm")
+        nc.vector.tensor_tensor(out=tabm[:], in0=tab[:].rearrange("p s q i -> p (s q) i"),
+                                in1=pick[:].unsqueeze(1).to_broadcast([P, 2 * NPOS, NFREQ]), op=ALU.mult)
+        cs = const.tile([P, 3 * NPOS], F32, name="cs")
+        nc.vector.tensor_reduce(out=cs[:, 0:2 * NPOS], in_=tabm[:], axis=AX.X, op=ALU.add)
+        nc.vector.tensor_scalar(out=cs[:, 2 * NPOS:3 * NPOS], in0=cs[:, NPOS:2 * NPOS], scalar1=-1.0, scalar2=None,
+                                op0=ALU.mult)
+        xc = []
+        xs = []
+        for T in range(4):
+            xc_T = const.tile([P, CHUNK], U32, name="xc%d" % T, align_bytes=64)
+            xs_T = const.tile([P, CHUNK], U8, name="xs%d" % T, align_bytes=64)
+            xc.append(xc_T)
+            xs.append(xs_T)
+
+        def x_widen(T, a2):
+            xt = psum.tile([P, 512], F32, name="xt", tag="bank")
+            for a in range(2):
+                t4 = 2 * a2 + a
+                xq = xwork.tile([P, KDIM], BF16, name="xq", bufs=4)
+                nc.vector.tensor_tensor(out=xq[:], in0=xb[T][:, t4 * KDIM:(t4 + 1) * KDIM].bitcast(FP8),
+                                        in1=sc[:], op=ALU.mult)
+                words = xq[:].bitcast(F32)
+                for u in range(2):
+                    nc.tensor.transpose(xt[:, (2 * a + u) * P:(2 * a + u + 1) * P], words[:, u:256:2], perm[:])
+            return xt
+
+        def x_copy(xt):
+            xg = xwork.tile([P, 1024], BF16, name="xg", align_bytes=64)
+            nc.scalar.copy(out=xg[:].bitcast(F32).rearrange("p (a m u) -> p a m u", a=2, u=2),
+                           in_=xt[:].rearrange("p (a u m) -> p a m u", a=2, u=2))
+            return xg
+
+        def x_quant(T, a2, xg):
+            nc.vector.quantize_mx(out=xc[T][:, a2 * 256:(a2 + 1) * 256].bitcast(FP8X4),
+                                  scales=xs[T][:, a2 * 256:(a2 + 1) * 256], in_=xg[:])
+
+        wc = []
+        ws = []
+        for part in range(3):
+            wc_p = const.tile([P, E], U32, name="wc%d" % part, align_bytes=64)
+            ws_p = const.tile([P, E], U8, name="ws%d" % part, align_bytes=64)
+            wc.append(wc_p)
+            ws.append(ws_p)
+
+        def w_lace_qk(part, g, on_act):
+            wg = wwork.tile([P, 2 * E], BF16, name="wgh", bufs=4, align_bytes=64)
+            src = wraw[part][:].rearrange("p t (h x) -> p h x t", x=HD)
+            for half in range(2):
+                f = 2 * g + half
+                dst = wg[:, half * 512:(half + 1) * 512].rearrange("p (h i t) -> p h i t", h=NH, i=NFREQ, t=4)
+                if on_act:
+                    nc.scalar.copy(out=dst, in_=src[:, :, f * 8:(f + 1) * 8, :])
+                else:
+                    nc.gpsimd.tensor_scalar(out=dst, in0=src[:, :, f * 8:(f + 1) * 8, :], scalar1=1.0, scalar2=0.0,
+                                            op0=ALU.mult, op1=ALU.add)
+            return wg
+
+        def w_quant_qk(part, g, wg):
+            nc.vector.quantize_mx(out=wc[part][:, g * 256:(g + 1) * 256].bitcast(FP8X4),
+                                  scales=ws[part][:, g * 256:(g + 1) * 256], in_=wg[:])
+
+        def w_lace_v():
+            wg = wwork.tile([P, 4 * E], BF16, name="wg", bufs=1, align_bytes=64)
+            nc.vector.tensor_copy(out=wg[:].rearrange("p (n t) -> p n t", t=4), in_=wraw[2][:].rearrange("p t n -> p n t"))
+            return wg
+
+        def mx(out, lc, ls, rc, rs):
+            nc.tensor.matmul_mx(out=out, lhsT=lc.bitcast(FP8X4), lhsT_scale=ls, rhs=rc.bitcast(FP8X4), rhs_scale=rs,
+                                start=True, stop=True)
+
+        def pair_of(s):
+            pq, rbit, ch = UNITS[s // 2]
+            return pq, rbit, ch, 1 - s % 2
+
+        def mx_pair(s):
+            pq, rbit, ch, g = pair_of(s)
+            T = 2 * rbit + ch
+            y = []
+            for half in range(2):
+                f = 2 * g + half
+                y_h = psum.tile([P, 512], F32, name="y%d" % half, tag="bank")
+                if s - 1 not in V_AT:
+                    mx(y_h[:], wc[0][:, 2 * P:3 * P], ws[0][:, 2 * P:3 * P], xc[0][:], xs[0][:])
+                mx(y_h[:], wc[pq][:, f * P:(f + 1) * P], ws[pq][:, f * P:(f + 1) * P], xc[T][:], xs[T][:])
+                y.append(y_h)
+            return y
+
+        def views(s):
+            pq, rbit, ch, g = pair_of(s)
+            if g == 1:
+                def yv(t, k):
+                    return t[:, k * P:(k + 1) * P]
+                return yv, yv, [4 * ch + k for k in range(4)]
+
+            def yr(t, k):
+                return t[:].rearrange("p (a w r) -> p r w a", a=4, w=32, r=4)[:, k]
+
+            def sr(t, k):
+                return t[:].rearrange("p (w r a) -> p r w a", w=32, r=4, a=4)[:, k]
+            return yr, sr, [2 * k + rbit for k in range(4)]
+
+        def first_products(s, y):
+            pq, rbit, ch, g = pair_of(s)
+            yv, sv, poss = views(s)
+            pt = []
+            ot = []
+            for half in range(2):
+                p_h = rot.tile([P, 512], F32, name="p%d%d" % (g, half))
+                o_h = rot.tile([P, 512], F32, name="o%d%d" % (g, half))
+                pt.append(p_h)
+                ot.append(o_h)
+            for half in range(2):
+                col = pq * 4 + 2 * g + half
+                for k in range(4):
+                    pos = poss[k]
+                    dst = sv(ot[half], k) if pos == 0 else sv(pt[half], k)
+                    if half == 1 and s in P_B_ON_V:
+                        nc.vector.tensor_scalar(out=dst, in0=yv(y[half], k), scalar1=cs[:, pos:pos + 1],
+                                                scalar2=rb[:, col, pos:pos + 1], op0=ALU.mult, op1=ALU.add)
+                    else:
+                        nc.scalar.activation(out=dst, in_=yv(y[half], k), func=ACTF.Identity,
+                                             bias=rb[:, col, pos:pos + 1], scale=cs[:, pos:pos + 1])
+            return pt, ot
+
+        def second_products(s, y, pt, ot):
+            yv, sv, poss = views(s)
+            for half in range(2):
+                soff = 2 * NPOS if half == 0 else NPOS
+                for k in range(4):
+                    pos = poss[k]
+                    if pos > 0:
+                        nc.vector.scalar_tensor_tensor(out=sv(ot[half], k), in0=yv(y[1 - half], k),
+                                                       scalar=cs[:, soff + pos:soff + pos + 1], in1=sv(pt[half], k),
+                                                       op0=ALU.mult, op1=ALU.add)
+
+        out_t = []
+        for part in range(3):
+            out_p = const.tile([P, NH, 2, NPOS, HD], F32, name="out%d" % part)
+            out_t.append(out_p)
+
+        def store(part, rbit, c0, c1):
+            dst = outs[part].rearrange("w h (rp rb c) d -> rp rb w h c d", rp=4, rb=2, c=8)
+            for rp in range(4):
+                nc.sync.dma_start(out=dst[rp, rbit, :, :, c0:c1, :].rearrange("w h c d -> w h (c d)"),
+                                  in_=out_t[part][rp:P:4, :, rbit, c0:c1, :].rearrange("p h c d -> p h (c d)"))
+
+        def turn_back(o0, o1, t4):
+            tr = psum.tile([P, 512], F32, name="tr", tag="bank")
+            for half in range(2):
+                nc.tensor.transpose(tr[:, half * P:(half + 1) * P], o0[half][:, t4:512:4], ident[:])
+            for half in range(2):
+                nc.tensor.transpose(tr[:, (2 + half) * P:(3 + half) * P], o1[half][:, t4 * P:(t4 + 1) * P], ident[:])
+            return tr
+
+        def copy_out(tr, u, t4):
+            pq, rbit, ch = UNITS[u]
+            dst = out_t[pq][:, :, rbit, 4 * ch + t4, :].rearrange("p h (f i) -> p h f i", f=4)
+            src = tr[:].rearrange("p (f h i) -> p h f i", f=4, h=NH, i=NFREQ)
+            if (u, t4) in EV_ON_V:
+                nc.vector.tensor_copy(out=dst, in_=src)
+            else:
+                nc.scalar.copy(out=dst, in_=src)
+
+        def v_mx(rbit, c):
+            T = 2 * rbit + c // 4
+            t4 = c % 4
+            yv_ = psum.tile([P, 512], F32, name="yv_", tag="bank")
+            mx(yv_[:], xc[T][:, t4 * P:(t4 + 1) * P], xs[T][:, t4 * P:(t4 + 1) * P], wc[2][:], ws[2][:])
+            return yv_
+
+        def v_add(yv_, rbit, c):
+            nc.vector.tensor_tensor(out=out_t[2][:, :, rbit, c, :], in0=yv_[:].rearrange("p (h d) -> p h d", d=HD),
+                                    in1=bv[:].rearrange("p (h d) -> p h d", d=HD), op=ALU.add)
+
+        wg_q1 = w_lace_qk(0, 1, False)
+        wg_k1 = w_lace_qk(1, 1, False)
+        wg_k0 = w_lace_qk(1, 0, False)
+        xt0 = x_widen(0, 0)
+        xt1 = x_widen(0, 1)
+        browf = const.tile([P, P], F32, name="browf")
+        nc.vector.tensor_copy(out=browf[:], in_=brow[:])
+        bps = psum.tile([P, 512], F32, name="bps", tag="bank")
+        nc.tensor.transpose(bps[:, 0:P], browf[:], ident[:])
+        bT = const.tile([P, 4, 2], F32, name="bT")
+        nc.vector.tensor_copy(out=bT[:].rearrange("p a b -> p (a b)"), in_=bps[:, 0:8])
+        bS = const.tile([P, 4, 2], F32, name="bS")
+        nc.vector.tensor_scalar(out=bS[:, :, 0], in0=bT[:, :, 1], scalar1=-1.0, scalar2=None, op0=ALU.mult)
+        nc.vector.tensor_copy(out=bS[:, :, 1], in_=bT[:, :, 0])
+        rb = const.tile([P, 8, NPOS], F32, name="rb")
+        rb2 = const.tile([P, 8, NPOS], F32, name="rb2")
+        nc.vector.tensor_tensor(out=rb2[:], in0=cs[:, 0:NPOS].unsqueeze(1).to_broadcast([P, 8, NPOS]),
+                                in1=bT[:].rearrange("p a b -> p (a b)").unsqueeze(2).to_broadcast([P, 8, NPOS]), op=ALU.mult)
+        nc.vector.tensor_tensor(out=rb[:], in0=cs[:, NPOS:2 * NPOS].unsqueeze(1).to_broadcast([P, 8, NPOS]),
+                                in1=bS[:].rearrange("p a b -> p (a b)").unsqueeze(2).to_broadcast([P, 8, NPOS]), op=ALU.mult)
+        nc.vector.tensor_tensor(out=rb[:], in0=rb[:], in1=rb2[:], op=ALU.add)
+
+        xg0 = x_copy(xt0)
+        xg1 = x_copy(xt1)
+        wg_q0 = w_lace_qk(0, 0, True)
+        warm = psum.tile([P, 512], F32, name="warm", tag="bank")
+        for wt in (xg0, xg1, wg_q1, wg_q0):
+            for hf in range(2):
+                nc.tensor.matmul(out=warm[:], lhsT=wt[:, 0:P], rhs=wt[:, hf * 512:(hf + 1) * 512], start=True, stop=True)
+        x_quant(0, 0, xg0)
+        w_quant_qk(0, 1, wg_q1)
+        x_quant(0, 1, xg1)
+        w_quant_qk(0, 0, wg_q0)
+        ys = {}
+        ys[0] = mx_pair(0)
+        ys[1] = mx_pair(1)
+        mx_done = 2
+        wg_v = w_lace_v()
+        w_quant_qk(1, 1, wg_k1)
+        nc.vector.quantize_mx(out=wc[2][:].bitcast(FP8X4), scales=ws[2][:], in_=wg_v[:])
+        w_quant_qk(1, 0, wg_k0)
+        pend_copy = []
+        pend_quant = []
+        chunk_ready = {0: 2, 1: 0, 2: 0, 3: 0}
+        pend_v = []
+        v_count = {0: 0, 1: 0}
+        ps_ = {}
+        os_ = {}
+        k_quant = False
+
+        for s in range(NPAIR + 3):
+            if 1 <= s <= NPAIR:
+                second_products(s - 1, ys[s - 1], ps_[s - 1], os_[s - 1])
+            for rbit, c, yv_ in pend_v:
+                v_add(yv_, rbit, c)
+                v_count[rbit] += 1
+                if V_HALF and v_count[rbit] % 4 == 0:
+                    store(2, rbit, v_count[rbit] - 4, v_count[rbit])
+                elif v_count[rbit] == NPOS:
+                    store(2, rbit, 0, NPOS)
+            pend_v = []
+            trs = []
+            if s >= 3:
+                u = (s - 3) // 2
+                for t4 in ((0, 1) if (s - 3) % 2 == 0 else (2, 3)):
+                    trs.append((u, t4, turn_back(os_[2 * u + 1], os_[2 * u], t4)))
+            if s < NPAIR:
+                ps_[s], os_[s] = first_products(s, ys[s])
+            for T, a2, xg in pend_quant:
+                x_quant(T, a2, xg)
+                chunk_ready[T] += 1
+            pend_quant = []
+            while mx_done < NPAIR and mx_done <= s + MX_LEAD:
+                npq, nrb, nch, ng = pair_of(mx_done)
+                if chunk_ready[2 * nrb + nch] < 2:
+                    break
+                ys[mx_done] = mx_pair(mx_done)
+                mx_done += 1
+            for u, t4, tr in trs:
+                copy_out(tr, u, t4)
+            for T, a2, xt in pend_copy:
+                pend_quant.append((T, a2, x_copy(xt)))
+            pend_copy = []
+            for T, a2 in XDEQ_AT.get(s, ()):
+                pend_copy.append((T, a2, x_widen(T, a2)))
+            for rbit, c in V_AT.get(s, ()):
+                pend_v.append((rbit, c, v_mx(rbit, c)))
+            if s >= 4 and (s - 4) % 2 == 0:
+                u = (s - 4) // 2
+                pq, rbit, ch = UNITS[u]
+                if u >= HALF_FROM:
+                    store(pq, rbit, 4 * ch, 4 * ch + 4)
+                elif ch == 1:
+                    store(pq, rbit, 0, NPOS)

@@ -25,7 +25,7 @@ E = 512
 KDIM = 512
 CHUNK = 512
 
-UNITS = [(pq, rb, ch) for rb in range(2) for ch in range(2) for pq in range(2)]
+UNITS = [(pq, 0, ch) for ch in range(2) for pq in range(2)] + [(pq, 1, ch) for pq in range(2) for ch in range(2)]
 NPAIR = 2 * len(UNITS)
 P_B_ON_V = frozenset((11, 15))
 EV_ON_V = frozenset(((7, 1), (7, 3)))

@@ -28,6 +28,7 @@ CHUNK = 512
 UNITS = [(pq, 0, ch) for ch in range(2) for pq in range(2)] + [(pq, 1, ch) for pq in range(2) for ch in range(2)]
 NPAIR = 2 * len(UNITS)
 P_B_ON_V = frozenset((11, 15))
+COL_ON_V = frozenset((0, 4, 8, 12, 14))
 EV_ON_V = frozenset(((7, 1), (7, 3)))
 V_AT = {0: ((0, 0), (0, 1)), 1: ((0, 2), (0, 3)), 4: ((0, 4), (0, 5)), 5: ((0, 6), (0, 7)), 7: ((1, 0), (1, 1)), 8: ((1, 2), (1, 3)), 10: ((1, 4), (1, 5)), 11: ((1, 6), (1, 7))}
 XDEQ_AT = {0: ((1, 0),), 1: ((1, 1),), 3: ((2, 0),), 4: ((2, 1),), 6: ((3, 0),), 7: ((3, 1),)}
@@ -72,8 +73,12 @@ def tile_hydra_attn_pa_kernel(tc, x_bytes, x_scale, qkv_w, qkv_b, out_0, out_1, 
         nc.sync.dma_start(out=sc[:], in_=x_scale.rearrange("a b c k -> (a b c k)").partition_broadcast(P))
         for q in range(2):
             nc.sync.dma_start(
-                out=brow[q * 4:(q + 1) * 4, :].rearrange("p (h i) -> p h i", i=NFREQ),
-                in_=qkv_b[q * E:(q + 1) * E].rearrange("(h f i) -> f h i", h=NH, f=4, i=NFREQ),
+                out=brow[q * 4:q * 4 + 2, :].rearrange("p (h i) -> p h i", i=NFREQ),
+                in_=qkv_b[q * E:(q + 1) * E].rearrange("(h f i) -> f h i", h=NH, f=4, i=NFREQ)[0:2],
+            )
+            nc.sync.dma_start(
+                out=brow[q * 4 + 2:q * 4 + 4, :].rearrange("p (h x) -> p h x", x=16),
+                in_=qkv_b[q * E:(q + 1) * E].rearrange("(a h x) -> a h x", a=2, x=HD)[:, :, 16:32],
             )
         load_w(0)
         load_w(1)
@@ -104,6 +109,14 @@ def tile_hydra_attn_pa_kernel(tc, x_bytes, x_scale, qkv_w, qkv_b, out_0, out_1, 
                                                 op1=ALU.add)
                     else:
                         nc.scalar.activation(out=dst, in_=zo[:], func=ACTF.Copy, bias=va, scale=vb - va)
+        same = const.tile([P, P], F32, name="same")
+        other = const.tile([P, P], F32, name="other")
+        ident_f = ident[:].rearrange("p (h f i) -> p f h i", h=8, f=2, i=NFREQ)
+        nc.gpsimd.tensor_scalar(out=same[:].rearrange("p (f h i) -> p f h i", f=2, h=8), in0=ident_f, scalar1=1.0,
+                                scalar2=0.0, op0=ALU.mult, op1=ALU.add)
+        for f in range(2):
+            nc.gpsimd.tensor_scalar(out=other[:, f * 64:(f + 1) * 64].rearrange("p (h i) -> p h i", h=8),
+                                    in0=ident_f[:, 1 - f], scalar1=1.0, scalar2=0.0, op0=ALU.mult, op1=ALU.add)
         perm = const.tile([P, P], F32, name="perm")
         nc.vector.tensor_copy(out=perm[:].rearrange("p (b j r) -> p b j r", b=16, j=2, r=4),
                               in_=ident[:].rearrange("p (b r j) -> p b j r", b=16, r=4, j=2))
@@ -112,10 +125,18 @@ def tile_hydra_attn_pa_kernel(tc, x_bytes, x_scale, qkv_w, qkv_b, out_0, out_1, 
         tabm = const.tile([P, 2 * NPOS, NFREQ], F32, name="tabm")
         nc.vector.tensor_tensor(out=tabm[:], in0=tab[:].rearrange("p s q i -> p (s q) i"),
                                 in1=pick[:].unsqueeze(1).to_broadcast([P, 2 * NPOS, NFREQ]), op=ALU.mult)
-        cs = const.tile([P, 3 * NPOS], F32, name="cs")
+        cs = const.tile([P, 4 * NPOS], F32, name="cs")
         nc.vector.tensor_reduce(out=cs[:, 0:2 * NPOS], in_=tabm[:], axis=AX.X, op=ALU.add)
         nc.vector.tensor_scalar(out=cs[:, 2 * NPOS:3 * NPOS], in0=cs[:, NPOS:2 * NPOS], scalar1=-1.0, scalar2=None,
                                 op0=ALU.mult)
+        halves = const.tile([P, 2], F32, name="halves")
+        nc.vector.tensor_reduce(out=halves[:], in_=ident[:].rearrange("p (h f i) -> p f h i", h=8, f=2, i=NFREQ), axis=AX.XY,
+                                op=ALU.add)
+        sign = const.tile([P, 1], F32, name="sign")
+        nc.vector.tensor_tensor(out=sign[:], in0=halves[:, 0:1], in1=halves[:, 1:2], op=ALU.subtract)
+        nc.vector.tensor_scalar(out=cs[:, 3 * NPOS:4 * NPOS], in0=cs[:, NPOS:2 * NPOS], scalar1=sign[:], scalar2=None,
+                                op0=ALU.mult)
+
         xc = []
         xs = []
         for T in range(4):
@@ -158,13 +179,17 @@ def tile_hydra_attn_pa_kernel(tc, x_bytes, x_scale, qkv_w, qkv_b, out_0, out_1, 
             wg = wwork.tile([P, 2 * E], BF16, name="wgh", bufs=4, align_bytes=64)
             src = wraw[part][:].rearrange("p t (h x) -> p h x t", x=HD)
             for half in range(2):
-                f = 2 * g + half
-                dst = wg[:, half * 512:(half + 1) * 512].rearrange("p (h i t) -> p h i t", h=NH, i=NFREQ, t=4)
-                if on_act:
-                    nc.scalar.copy(out=dst, in_=src[:, :, f * 8:(f + 1) * 8, :])
+                dst = wg[:, half * 512:(half + 1) * 512]
+                if g == 0:
+                    dst = dst.rearrange("p (h i t) -> p h i t", h=NH, i=NFREQ, t=4)
+                    part_src = src[:, :, half * 8:(half + 1) * 8, :]
                 else:
-                    nc.gpsimd.tensor_scalar(out=dst, in0=src[:, :, f * 8:(f + 1) * 8, :], scalar1=1.0, scalar2=0.0,
-                                            op0=ALU.mult, op1=ALU.add)
+                    dst = dst.rearrange("p (h x t) -> p h x t", h=8, x=16, t=4)
+                    part_src = src[:, half * 8:(half + 1) * 8, 16:32, :]
+                if on_act:
+                    nc.scalar.copy(out=dst, in_=part_src)
+                else:
+                    nc.gpsimd.tensor_scalar(out=dst, in0=part_src, scalar1=1.0, scalar2=0.0, op0=ALU.mult, op1=ALU.add)
             return wg
 
         def w_quant_qk(part, g, wg):
@@ -191,18 +216,12 @@ def tile_hydra_attn_pa_kernel(tc, x_bytes, x_scale, qkv_w, qkv_b, out_0, out_1, 
             for half in range(2):
                 f = 2 * g + half
                 y_h = psum.tile([P, 512], F32, name="y%d" % half, tag="bank")
-                if s - 1 not in V_AT:
-                    mx(y_h[:], wc[0][:, 2 * P:3 * P], ws[0][:, 2 * P:3 * P], xc[0][:], xs[0][:])
                 mx(y_h[:], wc[pq][:, f * P:(f + 1) * P], ws[pq][:, f * P:(f + 1) * P], xc[T][:], xs[T][:])
                 y.append(y_h)
             return y
 
         def views(s):
             pq, rbit, ch, g = pair_of(s)
-            if g == 1:
-                def yv(t, k):
-                    return t[:, k * P:(k + 1) * P]
-                return yv, yv, [4 * ch + k for k in range(4)]
 
             def yr(t, k):
                 return t[:].rearrange("p (a w r) -> p r w a", a=4, w=32, r=4)[:, k]
@@ -213,16 +232,35 @@ def tile_hydra_attn_pa_kernel(tc, x_bytes, x_scale, qkv_w, qkv_b, out_0, out_1, 
 
         def first_products(s, y):
             pq, rbit, ch, g = pair_of(s)
-            yv, sv, poss = views(s)
             pt = []
             ot = []
+            if g == 1:
+                yc = rot.tile([P, 2, 512], F32, name="yc")
+                zc = rot.tile([P, 2, 512], F32, name="zc")
+                for half in range(2):
+                    bias = bT[:, pq * 4 + 2 + half:pq * 4 + 3 + half]
+                    if half == 1 and s in COL_ON_V:
+                        nc.vector.tensor_scalar(out=yc[:, half, :], in0=y[half][:], scalar1=bias, scalar2=None, op0=ALU.add)
+                    else:
+                        nc.scalar.activation(out=yc[:, half, :], in_=y[half][:], func=ACTF.Identity, bias=bias, scale=1.0)
+                for k in range(4):
+                    pos = 4 * ch + k
+                    cols = slice(k * P, (k + 1) * P)
+                    if pos > 0:
+                        nc.gpsimd.tensor_scalar(out=zc[:, :, cols], in0=yc[:, :, cols],
+                                                scalar1=cs[:, 3 * NPOS + pos:3 * NPOS + pos + 1], scalar2=0.0,
+                                                op0=ALU.mult, op1=ALU.add)
+                        nc.gpsimd.tensor_scalar(out=yc[:, :, cols], in0=yc[:, :, cols], scalar1=cs[:, pos:pos + 1],
+                                                scalar2=0.0, op0=ALU.mult, op1=ALU.add)
+                return zc, yc
             for half in range(2):
-                p_h = rot.tile([P, 512], F32, name="p%d%d" % (g, half))
-                o_h = rot.tile([P, 512], F32, name="o%d%d" % (g, half))
+                p_h = rot.tile([P, 512], F32, name="p0%d" % half)
+                o_h = rot.tile([P, 512], F32, name="o0%d" % half)
                 pt.append(p_h)
                 ot.append(o_h)
+            yv, sv, poss = views(s)
             for half in range(2):
-                col = pq * 4 + 2 * g + half
+                col = pq * 2 + half
                 for k in range(4):
                     pos = poss[k]
                     dst = sv(ot[half], k) if pos == 0 else sv(pt[half], k)
@@ -235,6 +273,8 @@ def tile_hydra_attn_pa_kernel(tc, x_bytes, x_scale, qkv_w, qkv_b, out_0, out_1, 
             return pt, ot
 
         def second_products(s, y, pt, ot):
+            if pair_of(s)[3] == 1:
+                return
             yv, sv, poss = views(s)
             for half in range(2):
                 soff = 2 * NPOS if half == 0 else NPOS
@@ -256,12 +296,17 @@ def tile_hydra_attn_pa_kernel(tc, x_bytes, x_scale, qkv_w, qkv_b, out_0, out_1, 
                 nc.sync.dma_start(out=dst[rp, rbit, :, :, c0:c1, :].rearrange("w h c d -> w h (c d)"),
                                   in_=out_t[part][rp:P:4, :, rbit, c0:c1, :].rearrange("p h c d -> p h (c d)"))
 
-        def turn_back(o0, o1, t4):
+        def turn_back(o0, yc, zc, t4, pos):
             tr = psum.tile([P, 512], F32, name="tr", tag="bank")
             for half in range(2):
                 nc.tensor.transpose(tr[:, half * P:(half + 1) * P], o0[half][:, t4:512:4], ident[:])
+            cols = slice(t4 * P, (t4 + 1) * P)
             for half in range(2):
-                nc.tensor.transpose(tr[:, (2 + half) * P:(3 + half) * P], o1[half][:, t4 * P:(t4 + 1) * P], ident[:])
+                out = tr[:, 2 * P:4 * P].rearrange("p (f a x) -> p a f x", f=2, a=2)[:, half]
+                nc.tensor.matmul(out=out, lhsT=yc[:, half, cols], rhs=same[:], is_transpose=True, start=True, stop=pos == 0)
+                if pos > 0:
+                    nc.tensor.matmul(out=out, lhsT=zc[:, half, cols], rhs=other[:], is_transpose=True, start=False,
+                                     stop=True)
             return tr
 
         def copy_out(tr, u, t4):
@@ -293,26 +338,25 @@ def tile_hydra_attn_pa_kernel(tc, x_bytes, x_scale, qkv_w, qkv_b, out_0, out_1, 
         nc.vector.tensor_copy(out=browf[:], in_=brow[:])
         bps = psum.tile([P, 512], F32, name="bps", tag="bank")
         nc.tensor.transpose(bps[:, 0:P], browf[:], ident[:])
-        bT = const.tile([P, 4, 2], F32, name="bT")
-        nc.vector.tensor_copy(out=bT[:].rearrange("p a b -> p (a b)"), in_=bps[:, 0:8])
-        bS = const.tile([P, 4, 2], F32, name="bS")
-        nc.vector.tensor_scalar(out=bS[:, :, 0], in0=bT[:, :, 1], scalar1=-1.0, scalar2=None, op0=ALU.mult)
-        nc.vector.tensor_copy(out=bS[:, :, 1], in_=bT[:, :, 0])
-        rb = const.tile([P, 8, NPOS], F32, name="rb")
-        rb2 = const.tile([P, 8, NPOS], F32, name="rb2")
-        nc.vector.tensor_tensor(out=rb2[:], in0=cs[:, 0:NPOS].unsqueeze(1).to_broadcast([P, 8, NPOS]),
-                                in1=bT[:].rearrange("p a b -> p (a b)").unsqueeze(2).to_broadcast([P, 8, NPOS]), op=ALU.mult)
-        nc.vector.tensor_tensor(out=rb[:], in0=cs[:, NPOS:2 * NPOS].unsqueeze(1).to_broadcast([P, 8, NPOS]),
-                                in1=bS[:].rearrange("p a b -> p (a b)").unsqueeze(2).to_broadcast([P, 8, NPOS]), op=ALU.mult)
+        bT = const.tile([P, 8], F32, name="bT")
+        nc.vector.tensor_copy(out=bT[:], in_=bps[:, 0:8])
+        bT_q = bT[:].rearrange("p (q j) -> p q j", q=2)
+        bR = const.tile([P, 2, 2], F32, name="bR")
+        bS = const.tile([P, 2, 2], F32, name="bS")
+        nc.vector.tensor_copy(out=bR[:], in_=bT_q[:, :, 0:2])
+        nc.vector.tensor_scalar(out=bS[:, :, 0], in0=bT_q[:, :, 1], scalar1=-1.0, scalar2=None, op0=ALU.mult)
+        nc.vector.tensor_copy(out=bS[:, :, 1], in_=bT_q[:, :, 0])
+        rb = const.tile([P, 4, NPOS], F32, name="rb")
+        rb2 = const.tile([P, 4, NPOS], F32, name="rb2")
+        nc.vector.tensor_tensor(out=rb2[:], in0=cs[:, 0:NPOS].unsqueeze(1).to_broadcast([P, 4, NPOS]),
+                                in1=bR[:].rearrange("p a b -> p (a b)").unsqueeze(2).to_broadcast([P, 4, NPOS]), op=ALU.mult)
+        nc.vector.tensor_tensor(out=rb[:], in0=cs[:, NPOS:2 * NPOS].unsqueeze(1).to_broadcast([P, 4, NPOS]),
+                                in1=bS[:].rearrange("p a b -> p (a b)").unsqueeze(2).to_broadcast([P, 4, NPOS]), op=ALU.mult)
         nc.vector.tensor_tensor(out=rb[:], in0=rb[:], in1=rb2[:], op=ALU.add)
 
         xg0 = x_copy(xt0)
         xg1 = x_copy(xt1)
         wg_q0 = w_lace_qk(0, 0, True)
-        warm = psum.tile([P, 512], F32, name="warm", tag="bank")
-        for wt in (xg0, xg1, wg_q1, wg_q0):
-            for hf in range(2):
-                nc.tensor.matmul(out=warm[:], lhsT=wt[:, 0:P], rhs=wt[:, hf * 512:(hf + 1) * 512], start=True, stop=True)
         x_quant(0, 0, xg0)
         w_quant_qk(0, 1, wg_q1)
         x_quant(0, 1, xg1)
@@ -349,7 +393,7 @@ def tile_hydra_attn_pa_kernel(tc, x_bytes, x_scale, qkv_w, qkv_b, out_0, out_1, 
             if s >= 3:
                 u = (s - 3) // 2
                 for t4 in ((0, 1) if (s - 3) % 2 == 0 else (2, 3)):
-                    trs.append((u, t4, turn_back(os_[2 * u + 1], os_[2 * u], t4)))
+                    trs.append((u, t4, turn_back(os_[2 * u + 1], os_[2 * u], ps_[2 * u], t4, 4 * UNITS[u][2] + t4)))
             if s < NPAIR:
                 ps_[s], os_[s] = first_products(s, ys[s])
             for T, a2, xg in pend_quant:

@@ -27,14 +27,17 @@ CHUNK = 512
 
 UNITS = [(pq, 0, ch) for ch in range(2) for pq in range(2)] + [(pq, 1, ch) for pq in range(2) for ch in range(2)]
 NPAIR = 2 * len(UNITS)
+ON_GP = ((0, 1), (1, 1))
 P_B_ON_V = frozenset((11, 15))
-COL_ON_V = frozenset((0, 4, 8, 12, 14))
+Y_ON_V = frozenset((8, 10, 12, 14))
 EV_ON_V = frozenset(((7, 1), (7, 3)))
 V_AT = {0: ((0, 0), (0, 1)), 1: ((0, 2), (0, 3)), 4: ((0, 4), (0, 5)), 5: ((0, 6), (0, 7)), 7: ((1, 0), (1, 1)), 8: ((1, 2), (1, 3)), 10: ((1, 4), (1, 5)), 11: ((1, 6), (1, 7))}
 XDEQ_AT = {0: ((1, 0),), 1: ((1, 1),), 3: ((2, 0),), 4: ((2, 1),), 6: ((3, 0),), 7: ((3, 1),)}
-MX_LEAD = 1
-V_HALF = False
-HALF_FROM = 8
+MX_LEAD = 2
+LAG = 3
+LACE_K1 = 'A'
+LACE_K0 = 'A'
+LACE_V = 'V'
 
 
 def tile_hydra_attn_pa_kernel(tc, x_bytes, x_scale, qkv_w, qkv_b, out_0, out_1, out_2):
@@ -49,7 +52,6 @@ def tile_hydra_attn_pa_kernel(tc, x_bytes, x_scale, qkv_w, qkv_b, out_0, out_1, 
         psum = ctx.enter_context(tc.psum_pool(name="psum", bufs=8))
         ctx.enter_context(tc.manual_schedule())
 
-        sc = const.tile([P, KDIM], F32, name="sc")
         x_rows = x_bytes.rearrange("b (wi rp rb) (j c) k -> rb (b wi rp) j (c k)", wi=2, rp=4, rb=2, j=2)
         w_rows = qkv_w.rearrange("(p t) n -> p t n", t=4)
         xb = []
@@ -69,28 +71,48 @@ def tile_hydra_attn_pa_kernel(tc, x_bytes, x_scale, qkv_w, qkv_b, out_0, out_1, 
 
         brow = const.tile([P, P], BF16, name="brow")
         nc.vector.memset(brow[:], 0.0)
+        sc4 = const.tile([P, 4], F32, name="sc4")
+        bv4b = const.tile([P, 4], BF16, name="bv4b")
         load_x(0)
-        nc.sync.dma_start(out=sc[:], in_=x_scale.rearrange("a b c k -> (a b c k)").partition_broadcast(P))
+        nc.sync.dma_start(out=sc4[:], in_=x_scale.rearrange("a b c (p g) -> p (a b c g)", p=P, g=4))
         for q in range(2):
-            nc.sync.dma_start(
-                out=brow[q * 4:q * 4 + 2, :].rearrange("p (h i) -> p h i", i=NFREQ),
-                in_=qkv_b[q * E:(q + 1) * E].rearrange("(h f i) -> f h i", h=NH, f=4, i=NFREQ)[0:2],
-            )
-            nc.sync.dma_start(
-                out=brow[q * 4 + 2:q * 4 + 4, :].rearrange("p (h x) -> p h x", x=16),
-                in_=qkv_b[q * E:(q + 1) * E].rearrange("(a h x) -> a h x", a=2, x=HD)[:, :, 16:32],
-            )
+            bias_q = qkv_b[q * E:(q + 1) * E]
+            for g in range(2):
+                row = brow[q * 4 + 2 * g:q * 4 + 2 * g + 2, :]
+                if (q, g) in ON_GP:
+                    nc.sync.dma_start(out=row.rearrange("p (h x) -> p h x", x=16),
+                                      in_=bias_q.rearrange("(a h x) -> a h x", a=2, x=HD)[:, :, 16 * g:16 * g + 16])
+                else:
+                    nc.sync.dma_start(out=row.rearrange("p (h i) -> p h i", i=NFREQ),
+                                      in_=bias_q.rearrange("(h f i) -> f h i", h=NH, f=4, i=NFREQ)[2 * g:2 * g + 2])
         load_w(0)
         load_w(1)
         load_w(2)
-        bv = const.tile([P, E], BF16, name="bv")
-        nc.sync.dma_start(out=bv[:], in_=qkv_b[2 * E:3 * E].partition_broadcast(P))
+        nc.sync.dma_start(out=bv4b[:], in_=qkv_b[2 * E:3 * E].rearrange("(p g) -> p g", p=P, g=4))
         load_x(1)
         load_x(2)
         load_x(3)
 
         ident = const.tile([P, P], F32, name="ident")
         make_identity(nc, ident[:])
+        same = const.tile([P, P], F32, name="same")
+        other = const.tile([P, P], F32, name="other")
+        if ON_GP:
+            ident_f = ident[:].rearrange("p (h f i) -> p f h i", h=8, f=2, i=NFREQ)
+            nc.gpsimd.tensor_scalar(out=same[:].rearrange("p (f h i) -> p f h i", f=2, h=8), in0=ident_f, scalar1=1.0,
+                                    scalar2=0.0, op0=ALU.mult, op1=ALU.add)
+            for f in range(2):
+                nc.gpsimd.tensor_scalar(out=other[:, f * 64:(f + 1) * 64].rearrange("p (h i) -> p h i", h=8),
+                                        in0=ident_f[:, 1 - f], scalar1=1.0, scalar2=0.0, op0=ALU.mult, op1=ALU.add)
+        sc = const.tile([P, KDIM], F32, name="sc")
+        bv = const.tile([P, E], F32, name="bv")
+
+        def spread(dst, v4):
+            sp = psum.tile([P, 512], F32, name="sp", tag="bank")
+            for g in range(4):
+                nc.tensor.transpose(sp[:, g * P:(g + 1) * P], v4[:, g:g + 1].to_broadcast([P, P]), ident[:])
+            nc.scalar.copy(out=dst[:].rearrange("p (n g) -> p n g", g=4), in_=sp[:].rearrange("p (g n) -> p n g", g=4))
+
         zo = const.tile([P, 2], F32, name="zo")
         nc.vector.memset(zo[:, 0:1], 0.0)
         nc.vector.memset(zo[:, 1:2], 1.0)
@@ -109,14 +131,7 @@ def tile_hydra_attn_pa_kernel(tc, x_bytes, x_scale, qkv_w, qkv_b, out_0, out_1, 
                                                 op1=ALU.add)
                     else:
                         nc.scalar.activation(out=dst, in_=zo[:], func=ACTF.Copy, bias=va, scale=vb - va)
-        same = const.tile([P, P], F32, name="same")
-        other = const.tile([P, P], F32, name="other")
-        ident_f = ident[:].rearrange("p (h f i) -> p f h i", h=8, f=2, i=NFREQ)
-        nc.gpsimd.tensor_scalar(out=same[:].rearrange("p (f h i) -> p f h i", f=2, h=8), in0=ident_f, scalar1=1.0,
-                                scalar2=0.0, op0=ALU.mult, op1=ALU.add)
-        for f in range(2):
-            nc.gpsimd.tensor_scalar(out=other[:, f * 64:(f + 1) * 64].rearrange("p (h i) -> p h i", h=8),
-                                    in0=ident_f[:, 1 - f], scalar1=1.0, scalar2=0.0, op0=ALU.mult, op1=ALU.add)
+        spread(sc, sc4)
         perm = const.tile([P, P], F32, name="perm")
         nc.vector.tensor_copy(out=perm[:].rearrange("p (b j r) -> p b j r", b=16, j=2, r=4),
                               in_=ident[:].rearrange("p (b r j) -> p b j r", b=16, r=4, j=2))
@@ -129,13 +144,14 @@ def tile_hydra_attn_pa_kernel(tc, x_bytes, x_scale, qkv_w, qkv_b, out_0, out_1, 
         nc.vector.tensor_reduce(out=cs[:, 0:2 * NPOS], in_=tabm[:], axis=AX.X, op=ALU.add)
         nc.vector.tensor_scalar(out=cs[:, 2 * NPOS:3 * NPOS], in0=cs[:, NPOS:2 * NPOS], scalar1=-1.0, scalar2=None,
                                 op0=ALU.mult)
-        halves = const.tile([P, 2], F32, name="halves")
-        nc.vector.tensor_reduce(out=halves[:], in_=ident[:].rearrange("p (h f i) -> p f h i", h=8, f=2, i=NFREQ), axis=AX.XY,
-                                op=ALU.add)
-        sign = const.tile([P, 1], F32, name="sign")
-        nc.vector.tensor_tensor(out=sign[:], in0=halves[:, 0:1], in1=halves[:, 1:2], op=ALU.subtract)
-        nc.vector.tensor_scalar(out=cs[:, 3 * NPOS:4 * NPOS], in0=cs[:, NPOS:2 * NPOS], scalar1=sign[:], scalar2=None,
-                                op0=ALU.mult)
+        if ON_GP:
+            halves = const.tile([P, 2], F32, name="halves")
+            nc.vector.tensor_reduce(out=halves[:], in_=ident[:].rearrange("p (h f i) -> p f h i", h=8, f=2, i=NFREQ),
+                                    axis=AX.XY, op=ALU.add)
+            sign = const.tile([P, 1], F32, name="sign")
+            nc.vector.tensor_tensor(out=sign[:], in0=halves[:, 0:1], in1=halves[:, 1:2], op=ALU.subtract)
+            nc.vector.tensor_scalar(out=cs[:, 3 * NPOS:4 * NPOS], in0=cs[:, NPOS:2 * NPOS], scalar1=sign[:], scalar2=None,
+                                    op0=ALU.mult)
 
         xc = []
         xs = []
@@ -175,30 +191,37 @@ def tile_hydra_attn_pa_kernel(tc, x_bytes, x_scale, qkv_w, qkv_b, out_0, out_1, 
             wc.append(wc_p)
             ws.append(ws_p)
 
-        def w_lace_qk(part, g, on_act):
+        def lace(eng, dst, src):
+            if eng == 'A':
+                nc.scalar.copy(out=dst, in_=src)
+            elif eng == 'V':
+                nc.vector.tensor_copy(out=dst, in_=src)
+            else:
+                nc.gpsimd.tensor_scalar(out=dst, in0=src, scalar1=1.0, scalar2=0.0, op0=ALU.mult, op1=ALU.add)
+
+        def w_lace_qk(part, g, eng):
             wg = wwork.tile([P, 2 * E], BF16, name="wgh", bufs=4, align_bytes=64)
             src = wraw[part][:].rearrange("p t (h x) -> p h x t", x=HD)
             for half in range(2):
                 dst = wg[:, half * 512:(half + 1) * 512]
-                if g == 0:
-                    dst = dst.rearrange("p (h i t) -> p h i t", h=NH, i=NFREQ, t=4)
-                    part_src = src[:, :, half * 8:(half + 1) * 8, :]
+                if (part, g) in ON_GP:
+                    lace(eng, dst.rearrange("p (h x t) -> p h x t", h=8, x=16, t=4),
+                         src[:, half * 8:(half + 1) * 8, 16 * g:16 * g + 16, :])
                 else:
-                    dst = dst.rearrange("p (h x t) -> p h x t", h=8, x=16, t=4)
-                    part_src = src[:, half * 8:(half + 1) * 8, 16:32, :]
-                if on_act:
-                    nc.scalar.copy(out=dst, in_=part_src)
-                else:
-                    nc.gpsimd.tensor_scalar(out=dst, in0=part_src, scalar1=1.0, scalar2=0.0, op0=ALU.mult, op1=ALU.add)
+                    f = 2 * g + half
+                    lace(eng, dst.rearrange("p (h i t) -> p h i t", h=NH, i=NFREQ, t=4), src[:, :, f * 8:(f + 1) * 8, :])
             return wg
 
         def w_quant_qk(part, g, wg):
             nc.vector.quantize_mx(out=wc[part][:, g * 256:(g + 1) * 256].bitcast(FP8X4),
                                   scales=ws[part][:, g * 256:(g + 1) * 256], in_=wg[:])
 
-        def w_lace_v():
+        def w_lace_v(eng):
             wg = wwork.tile([P, 4 * E], BF16, name="wg", bufs=1, align_bytes=64)
-            nc.vector.tensor_copy(out=wg[:].rearrange("p (n t) -> p n t", t=4), in_=wraw[2][:].rearrange("p t n -> p n t"))
+            n = E // 4
+            for c in range(4):
+                lace(eng, wg[:, c * 4 * n:(c + 1) * 4 * n].rearrange("p (n t) -> p n t", t=4),
+                     wraw[2][:, :, c * n:(c + 1) * n].rearrange("p t n -> p n t"))
             return wg
 
         def mx(out, lc, ls, rc, rs):
@@ -220,93 +243,112 @@ def tile_hydra_attn_pa_kernel(tc, x_bytes, x_scale, qkv_w, qkv_b, out_0, out_1, 
                 y.append(y_h)
             return y
 
-        def views(s):
+        def psum_view(t, g, k):
+            if g == 1:
+                return t[:, k * P:(k + 1) * P]
+            return t[:].rearrange("p (a w r) -> p r w a", a=4, w=32, r=4)[:, k]
+
+        def sbuf_view(t, g, k):
+            if g == 1:
+                return t[:, k * P:(k + 1) * P]
+            return t[:].rearrange("p (w r a) -> p r w a", w=32, r=4, a=4)[:, k]
+
+        def position(s, k):
             pq, rbit, ch, g = pair_of(s)
-
-            def yr(t, k):
-                return t[:].rearrange("p (a w r) -> p r w a", a=4, w=32, r=4)[:, k]
-
-            def sr(t, k):
-                return t[:].rearrange("p (w r a) -> p r w a", w=32, r=4, a=4)[:, k]
-            return yr, sr, [2 * k + rbit for k in range(4)]
+            return 4 * ch + k if g == 1 else 2 * k + rbit
 
         def first_products(s, y):
             pq, rbit, ch, g = pair_of(s)
+            if (pq, g) in ON_GP:
+                yc = rot.tile([P, 2, 512], F32, name="yc%d" % g, bufs=4)
+                zc = rot.tile([P, 2, 512], F32, name="zc%d" % g, bufs=4)
+                for half in range(2):
+                    bias = bT[:, pq, 2 * g + half:2 * g + half + 1]
+                    if g == 1:
+                        dst, src = yc[:, half, :], y[half][:]
+                    else:
+                        dst = yc[:, half, :].rearrange("p (w r a) -> p w r a", w=32, r=4, a=4)
+                        src = y[half][:].rearrange("p (a w r) -> p w r a", a=4, w=32, r=4)
+                    if half == 1 and s in Y_ON_V:
+                        nc.vector.tensor_scalar(out=dst, in0=src, scalar1=bias, scalar2=None, op0=ALU.add)
+                    else:
+                        nc.scalar.activation(out=dst, in_=src, func=ACTF.Identity, bias=bias, scale=1.0)
+                for k in range(4):
+                    pos = position(s, k)
+                    if g == 1:
+                        yk, zk = yc[:, :, k * P:(k + 1) * P], zc[:, :, k * P:(k + 1) * P]
+                    else:
+                        yk = yc[:].rearrange("p b (w r a) -> p r b w a", w=32, r=4, a=4)[:, k]
+                        zk = zc[:].rearrange("p b (w r a) -> p r b w a", w=32, r=4, a=4)[:, k]
+                    if pos > 0 or g == 0:
+                        nc.gpsimd.tensor_scalar(out=zk, in0=yk, scalar1=cs[:, 3 * NPOS + pos:3 * NPOS + pos + 1],
+                                                scalar2=0.0, op0=ALU.mult, op1=ALU.add)
+                    if pos > 0:
+                        nc.gpsimd.tensor_scalar(out=yk, in0=yk, scalar1=cs[:, pos:pos + 1], scalar2=0.0, op0=ALU.mult,
+                                                op1=ALU.add)
+                return zc, yc
             pt = []
             ot = []
-            if g == 1:
-                yc = rot.tile([P, 2, 512], F32, name="yc")
-                zc = rot.tile([P, 2, 512], F32, name="zc")
-                for half in range(2):
-                    bias = bT[:, pq * 4 + 2 + half:pq * 4 + 3 + half]
-                    if half == 1 and s in COL_ON_V:
-                        nc.vector.tensor_scalar(out=yc[:, half, :], in0=y[half][:], scalar1=bias, scalar2=None, op0=ALU.add)
-                    else:
-                        nc.scalar.activation(out=yc[:, half, :], in_=y[half][:], func=ACTF.Identity, bias=bias, scale=1.0)
-                for k in range(4):
-                    pos = 4 * ch + k
-                    cols = slice(k * P, (k + 1) * P)
-                    if pos > 0:
-                        nc.gpsimd.tensor_scalar(out=zc[:, :, cols], in0=yc[:, :, cols],
-                                                scalar1=cs[:, 3 * NPOS + pos:3 * NPOS + pos + 1], scalar2=0.0,
-                                                op0=ALU.mult, op1=ALU.add)
-                        nc.gpsimd.tensor_scalar(out=yc[:, :, cols], in0=yc[:, :, cols], scalar1=cs[:, pos:pos + 1],
-                                                scalar2=0.0, op0=ALU.mult, op1=ALU.add)
-                return zc, yc
             for half in range(2):
-                p_h = rot.tile([P, 512], F32, name="p0%d" % half)
-                o_h = rot.tile([P, 512], F32, name="o0%d" % half)
+                p_h = rot.tile([P, 512], F32, name="p%d%d" % (g, half))
+                o_h = rot.tile([P, 512], F32, name="o%d%d" % (g, half))
                 pt.append(p_h)
                 ot.append(o_h)
-            yv, sv, poss = views(s)
             for half in range(2):
-                col = pq * 2 + half
+                col = pq * 4 + 2 * g + half
                 for k in range(4):
-                    pos = poss[k]
-                    dst = sv(ot[half], k) if pos == 0 else sv(pt[half], k)
+                    pos = position(s, k)
+                    dst = sbuf_view(ot[half] if pos == 0 else pt[half], g, k)
+                    src = psum_view(y[half], g, k)
                     if half == 1 and s in P_B_ON_V:
-                        nc.vector.tensor_scalar(out=dst, in0=yv(y[half], k), scalar1=cs[:, pos:pos + 1],
+                        nc.vector.tensor_scalar(out=dst, in0=src, scalar1=cs[:, pos:pos + 1],
                                                 scalar2=rb[:, col, pos:pos + 1], op0=ALU.mult, op1=ALU.add)
                     else:
-                        nc.scalar.activation(out=dst, in_=yv(y[half], k), func=ACTF.Identity,
-                                             bias=rb[:, col, pos:pos + 1], scale=cs[:, pos:pos + 1])
+                        nc.scalar.activation(out=dst, in_=src, func=ACTF.Identity, bias=rb[:, col, pos:pos + 1],
+                                             scale=cs[:, pos:pos + 1])
             return pt, ot
 
         def second_products(s, y, pt, ot):
-            if pair_of(s)[3] == 1:
+            pq, rbit, ch, g = pair_of(s)
+            if (pq, g) in ON_GP:
                 return
-            yv, sv, poss = views(s)
             for half in range(2):
                 soff = 2 * NPOS if half == 0 else NPOS
                 for k in range(4):
-                    pos = poss[k]
+                    pos = position(s, k)
                     if pos > 0:
-                        nc.vector.scalar_tensor_tensor(out=sv(ot[half], k), in0=yv(y[1 - half], k),
-                                                       scalar=cs[:, soff + pos:soff + pos + 1], in1=sv(pt[half], k),
-                                                       op0=ALU.mult, op1=ALU.add)
+                        nc.vector.scalar_tensor_tensor(out=sbuf_view(ot[half], g, k), in0=psum_view(y[1 - half], g, k),
+                                                       scalar=cs[:, soff + pos:soff + pos + 1],
+                                                       in1=sbuf_view(pt[half], g, k), op0=ALU.mult, op1=ALU.add)
 
         out_t = []
         for part in range(3):
             out_p = const.tile([P, NH, 2, NPOS, HD], F32, name="out%d" % part)
             out_t.append(out_p)
 
-        def store(part, rbit, c0, c1):
+        def store(part, rbit):
             dst = outs[part].rearrange("w h (rp rb c) d -> rp rb w h c d", rp=4, rb=2, c=8)
             for rp in range(4):
-                nc.sync.dma_start(out=dst[rp, rbit, :, :, c0:c1, :].rearrange("w h c d -> w h (c d)"),
-                                  in_=out_t[part][rp:P:4, :, rbit, c0:c1, :].rearrange("p h c d -> p h (c d)"))
+                nc.sync.dma_start(out=dst[rp, rbit].rearrange("w h c d -> w h (c d)"),
+                                  in_=out_t[part][rp:P:4, :, rbit].rearrange("p h c d -> p h (c d)"))
 
-        def turn_back(o0, yc, zc, t4, pos):
+        def turn_back(u, t4):
+            pq, rbit, ch = UNITS[u]
             tr = psum.tile([P, 512], F32, name="tr", tag="bank")
-            for half in range(2):
-                nc.tensor.transpose(tr[:, half * P:(half + 1) * P], o0[half][:, t4:512:4], ident[:])
-            cols = slice(t4 * P, (t4 + 1) * P)
-            for half in range(2):
-                out = tr[:, 2 * P:4 * P].rearrange("p (f a x) -> p a f x", f=2, a=2)[:, half]
-                nc.tensor.matmul(out=out, lhsT=yc[:, half, cols], rhs=same[:], is_transpose=True, start=True, stop=pos == 0)
-                if pos > 0:
-                    nc.tensor.matmul(out=out, lhsT=zc[:, half, cols], rhs=other[:], is_transpose=True, start=False,
-                                     stop=True)
+            for g in range(2):
+                cols = slice(t4 * P, (t4 + 1) * P) if g == 1 else slice(t4, 512, 4)
+                a, b = ps_[2 * u + 1 - g], os_[2 * u + 1 - g]
+                for half in range(2):
+                    if (pq, g) in ON_GP:
+                        out = tr[:, g * 256:(g + 1) * 256].rearrange("p (f b x) -> p b f x", f=2, b=2)[:, half]
+                        one = g == 1 and position(2 * u, t4) == 0
+                        nc.tensor.matmul(out=out, lhsT=b[:, half, cols], rhs=same[:], is_transpose=True, start=True, stop=one)
+                        if not one:
+                            nc.tensor.matmul(out=out, lhsT=a[:, half, cols], rhs=other[:], is_transpose=True, start=False,
+                                             stop=True)
+                    else:
+                        f = 2 * g + half
+                        nc.tensor.transpose(tr[:, f * P:(f + 1) * P], b[half][:, cols], ident[:])
             return tr
 
         def copy_out(tr, u, t4):
@@ -329,44 +371,47 @@ def tile_hydra_attn_pa_kernel(tc, x_bytes, x_scale, qkv_w, qkv_b, out_0, out_1, 
             nc.vector.tensor_tensor(out=out_t[2][:, :, rbit, c, :], in0=yv_[:].rearrange("p (h d) -> p h d", d=HD),
                                     in1=bv[:].rearrange("p (h d) -> p h d", d=HD), op=ALU.add)
 
-        wg_q1 = w_lace_qk(0, 1, False)
-        wg_k1 = w_lace_qk(1, 1, False)
-        wg_k0 = w_lace_qk(1, 0, False)
-        xt0 = x_widen(0, 0)
-        xt1 = x_widen(0, 1)
+        wg_q1 = w_lace_qk(0, 1, 'G')
+        wg_q0 = w_lace_qk(0, 0, 'A')
+        if LACE_V == 'G':
+            wg_v = w_lace_v('G')
+        wg_k1 = w_lace_qk(1, 1, LACE_K1)
         browf = const.tile([P, P], F32, name="browf")
         nc.vector.tensor_copy(out=browf[:], in_=brow[:])
         bps = psum.tile([P, 512], F32, name="bps", tag="bank")
         nc.tensor.transpose(bps[:, 0:P], browf[:], ident[:])
-        bT = const.tile([P, 8], F32, name="bT")
-        nc.vector.tensor_copy(out=bT[:], in_=bps[:, 0:8])
-        bT_q = bT[:].rearrange("p (q j) -> p q j", q=2)
-        bR = const.tile([P, 2, 2], F32, name="bR")
-        bS = const.tile([P, 2, 2], F32, name="bS")
-        nc.vector.tensor_copy(out=bR[:], in_=bT_q[:, :, 0:2])
-        nc.vector.tensor_scalar(out=bS[:, :, 0], in0=bT_q[:, :, 1], scalar1=-1.0, scalar2=None, op0=ALU.mult)
-        nc.vector.tensor_copy(out=bS[:, :, 1], in_=bT_q[:, :, 0])
-        rb = const.tile([P, 4, NPOS], F32, name="rb")
-        rb2 = const.tile([P, 4, NPOS], F32, name="rb2")
-        nc.vector.tensor_tensor(out=rb2[:], in0=cs[:, 0:NPOS].unsqueeze(1).to_broadcast([P, 4, NPOS]),
-                                in1=bR[:].rearrange("p a b -> p (a b)").unsqueeze(2).to_broadcast([P, 4, NPOS]), op=ALU.mult)
-        nc.vector.tensor_tensor(out=rb[:], in0=cs[:, NPOS:2 * NPOS].unsqueeze(1).to_broadcast([P, 4, NPOS]),
-                                in1=bS[:].rearrange("p a b -> p (a b)").unsqueeze(2).to_broadcast([P, 4, NPOS]), op=ALU.mult)
-        nc.vector.tensor_tensor(out=rb[:], in0=rb[:], in1=rb2[:], op=ALU.add)
-
+        xt0 = x_widen(0, 0)
+        xt1 = x_widen(0, 1)
         xg0 = x_copy(xt0)
         xg1 = x_copy(xt1)
-        wg_q0 = w_lace_qk(0, 0, True)
+        wg_k0 = w_lace_qk(1, 0, LACE_K0)
         x_quant(0, 0, xg0)
         w_quant_qk(0, 1, wg_q1)
+        bT = const.tile([P, 2, 4], F32, name="bT")
+        nc.vector.tensor_copy(out=bT[:].rearrange("p a b -> p (a b)"), in_=bps[:, 0:8])
+        bS = const.tile([P, 4, 2], F32, name="bS")
+        bT2 = bT[:].rearrange("p a (b c) -> p (a b) c", c=2)
+        nc.vector.tensor_scalar(out=bS[:, :, 0], in0=bT2[:, :, 1], scalar1=-1.0, scalar2=None, op0=ALU.mult)
+        nc.vector.tensor_copy(out=bS[:, :, 1], in_=bT2[:, :, 0])
+        rb = const.tile([P, 8, NPOS], F32, name="rb")
+        rb2 = const.tile([P, 8, NPOS], F32, name="rb2")
+        nc.vector.tensor_tensor(out=rb2[:], in0=cs[:, 0:NPOS].unsqueeze(1).to_broadcast([P, 8, NPOS]),
+                                in1=bT[:].rearrange("p a b -> p (a b)").unsqueeze(2).to_broadcast([P, 8, NPOS]), op=ALU.mult)
+        nc.vector.tensor_tensor(out=rb[:], in0=cs[:, NPOS:2 * NPOS].unsqueeze(1).to_broadcast([P, 8, NPOS]),
+                                in1=bS[:].rearrange("p a b -> p (a b)").unsqueeze(2).to_broadcast([P, 8, NPOS]), op=ALU.mult)
+        nc.vector.tensor_tensor(out=rb[:], in0=rb[:], in1=rb2[:], op=ALU.add)
         x_quant(0, 1, xg1)
         w_quant_qk(0, 0, wg_q0)
         ys = {}
         ys[0] = mx_pair(0)
         ys[1] = mx_pair(1)
         mx_done = 2
-        wg_v = w_lace_v()
         w_quant_qk(1, 1, wg_k1)
+        bv4 = const.tile([P, 4], F32, name="bv4")
+        nc.vector.tensor_copy(out=bv4[:], in_=bv4b[:])
+        spread(bv, bv4)
+        if LACE_V != 'G':
+            wg_v = w_lace_v(LACE_V)
         nc.vector.quantize_mx(out=wc[2][:].bitcast(FP8X4), scales=ws[2][:], in_=wg_v[:])
         w_quant_qk(1, 0, wg_k0)
         pend_copy = []
@@ -376,24 +421,21 @@ def tile_hydra_attn_pa_kernel(tc, x_bytes, x_scale, qkv_w, qkv_b, out_0, out_1, 
         v_count = {0: 0, 1: 0}
         ps_ = {}
         os_ = {}
-        k_quant = False
 
-        for s in range(NPAIR + 3):
+        for s in range(NPAIR + LAG):
             if 1 <= s <= NPAIR:
                 second_products(s - 1, ys[s - 1], ps_[s - 1], os_[s - 1])
             for rbit, c, yv_ in pend_v:
                 v_add(yv_, rbit, c)
                 v_count[rbit] += 1
-                if V_HALF and v_count[rbit] % 4 == 0:
-                    store(2, rbit, v_count[rbit] - 4, v_count[rbit])
-                elif v_count[rbit] == NPOS:
-                    store(2, rbit, 0, NPOS)
+                if v_count[rbit] == NPOS:
+                    store(2, rbit)
             pend_v = []
             trs = []
-            if s >= 3:
-                u = (s - 3) // 2
-                for t4 in ((0, 1) if (s - 3) % 2 == 0 else (2, 3)):
-                    trs.append((u, t4, turn_back(os_[2 * u + 1], os_[2 * u], ps_[2 * u], t4, 4 * UNITS[u][2] + t4)))
+            if s >= LAG:
+                u = (s - LAG) // 2
+                for t4 in ((0, 1) if (s - LAG) % 2 == 0 else (2, 3)):
+                    trs.append((u, t4, turn_back(u, t4)))
             if s < NPAIR:
                 ps_[s], os_[s] = first_products(s, ys[s])
             for T, a2, xg in pend_quant:
@@ -406,6 +448,8 @@ def tile_hydra_attn_pa_kernel(tc, x_bytes, x_scale, qkv_w, qkv_b, out_0, out_1, 
                     break
                 ys[mx_done] = mx_pair(mx_done)
                 mx_done += 1
+            for rbit, c in V_AT.get(s, ()):
+                pend_v.append((rbit, c, v_mx(rbit, c)))
             for u, t4, tr in trs:
                 copy_out(tr, u, t4)
             for T, a2, xt in pend_copy:
@@ -413,12 +457,7 @@ def tile_hydra_attn_pa_kernel(tc, x_bytes, x_scale, qkv_w, qkv_b, out_0, out_1, 
             pend_copy = []
             for T, a2 in XDEQ_AT.get(s, ()):
                 pend_copy.append((T, a2, x_widen(T, a2)))
-            for rbit, c in V_AT.get(s, ()):
-                pend_v.append((rbit, c, v_mx(rbit, c)))
-            if s >= 4 and (s - 4) % 2 == 0:
-                u = (s - 4) // 2
-                pq, rbit, ch = UNITS[u]
-                if u >= HALF_FROM:
-                    store(pq, rbit, 4 * ch, 4 * ch + 4)
-                elif ch == 1:
-                    store(pq, rbit, 0, NPOS)
+            if s > LAG and (s - LAG) % 2 == 1:
+                u = (s - LAG) // 2
+                if UNITS[u][2] == 1:
+                    store(UNITS[u][0], UNITS[u][1])

@@ -27,17 +27,18 @@ CHUNK = 512
 
 UNITS = [(pq, 0, ch) for ch in range(2) for pq in range(2)] + [(pq, 1, ch) for pq in range(2) for ch in range(2)]
 NPAIR = 2 * len(UNITS)
-ON_GP = ((0, 1), (1, 1))
+ON_GP = ((1, 1),)
 P_B_ON_V = frozenset((11, 15))
 Y_ON_V = frozenset((8, 10, 12, 14))
 EV_ON_V = frozenset(((7, 1), (7, 3)))
 V_AT = {0: ((0, 0), (0, 1)), 1: ((0, 2), (0, 3)), 4: ((0, 4), (0, 5)), 5: ((0, 6), (0, 7)), 7: ((1, 0), (1, 1)), 8: ((1, 2), (1, 3)), 10: ((1, 4), (1, 5)), 11: ((1, 6), (1, 7))}
 XDEQ_AT = {0: ((1, 0),), 1: ((1, 1),), 3: ((2, 0),), 4: ((2, 1),), 6: ((3, 0),), 7: ((3, 1),)}
 MX_LEAD = 2
+V_PARTS = 4
 LAG = 3
 LACE_K1 = 'A'
 LACE_K0 = 'A'
-LACE_V = 'V'
+LACE_V = 'G'
 
 
 def tile_hydra_attn_pa_kernel(tc, x_bytes, x_scale, qkv_w, qkv_b, out_0, out_1, out_2):
@@ -73,8 +74,8 @@ def tile_hydra_attn_pa_kernel(tc, x_bytes, x_scale, qkv_w, qkv_b, out_0, out_1, 
         nc.vector.memset(brow[:], 0.0)
         sc4 = const.tile([P, 4], F32, name="sc4")
         bv4b = const.tile([P, 4], BF16, name="bv4b")
-        load_x(0)
         nc.sync.dma_start(out=sc4[:], in_=x_scale.rearrange("a b c (p g) -> p (a b c g)", p=P, g=4))
+        load_x(0)
         for q in range(2):
             bias_q = qkv_b[q * E:(q + 1) * E]
             for g in range(2):
@@ -107,10 +108,13 @@ def tile_hydra_attn_pa_kernel(tc, x_bytes, x_scale, qkv_w, qkv_b, out_0, out_1, 
         sc = const.tile([P, KDIM], F32, name="sc")
         bv = const.tile([P, E], F32, name="bv")
 
-        def spread(dst, v4):
+        def spread(v4):
             sp = psum.tile([P, 512], F32, name="sp", tag="bank")
             for g in range(4):
                 nc.tensor.transpose(sp[:, g * P:(g + 1) * P], v4[:, g:g + 1].to_broadcast([P, P]), ident[:])
+            return sp
+
+        def spread_out(dst, sp):
             nc.scalar.copy(out=dst[:].rearrange("p (n g) -> p n g", g=4), in_=sp[:].rearrange("p (g n) -> p n g", g=4))
 
         zo = const.tile([P, 2], F32, name="zo")
@@ -131,7 +135,7 @@ def tile_hydra_attn_pa_kernel(tc, x_bytes, x_scale, qkv_w, qkv_b, out_0, out_1, 
                                                 op1=ALU.add)
                     else:
                         nc.scalar.activation(out=dst, in_=zo[:], func=ACTF.Copy, bias=va, scale=vb - va)
-        spread(sc, sc4)
+        spread_out(sc, spread(sc4))
         perm = const.tile([P, P], F32, name="perm")
         nc.vector.tensor_copy(out=perm[:].rearrange("p (b j r) -> p b j r", b=16, j=2, r=4),
                               in_=ident[:].rearrange("p (b r j) -> p b j r", b=16, r=4, j=2))
@@ -218,8 +222,8 @@ def tile_hydra_attn_pa_kernel(tc, x_bytes, x_scale, qkv_w, qkv_b, out_0, out_1, 
 
         def w_lace_v(eng):
             wg = wwork.tile([P, 4 * E], BF16, name="wg", bufs=1, align_bytes=64)
-            n = E // 4
-            for c in range(4):
+            n = E // V_PARTS
+            for c in range(V_PARTS):
                 lace(eng, wg[:, c * 4 * n:(c + 1) * 4 * n].rearrange("p (n t) -> p n t", t=4),
                      wraw[2][:, :, c * n:(c + 1) * n].rearrange("p t n -> p n t"))
             return wg
@@ -260,8 +264,8 @@ def tile_hydra_attn_pa_kernel(tc, x_bytes, x_scale, qkv_w, qkv_b, out_0, out_1, 
         def first_products(s, y):
             pq, rbit, ch, g = pair_of(s)
             if (pq, g) in ON_GP:
-                yc = rot.tile([P, 2, 512], F32, name="yc%d" % g, bufs=4)
-                zc = rot.tile([P, 2, 512], F32, name="zc%d" % g, bufs=4)
+                yc = rot.tile([P, 2, 512], F32, name="yc%d" % g, bufs=3)
+                zc = rot.tile([P, 2, 512], F32, name="zc%d" % g, bufs=3)
                 for half in range(2):
                     bias = bT[:, pq, 2 * g + half:2 * g + half + 1]
                     if g == 1:
@@ -385,10 +389,19 @@ def tile_hydra_attn_pa_kernel(tc, x_bytes, x_scale, qkv_w, qkv_b, out_0, out_1, 
         xg0 = x_copy(xt0)
         xg1 = x_copy(xt1)
         wg_k0 = w_lace_qk(1, 0, LACE_K0)
+        bv4 = const.tile([P, 4], F32, name="bv4")
+        nc.vector.tensor_copy(out=bv4[:], in_=bv4b[:])
+        bvp = spread(bv4)
         x_quant(0, 0, xg0)
         w_quant_qk(0, 1, wg_q1)
         bT = const.tile([P, 2, 4], F32, name="bT")
         nc.vector.tensor_copy(out=bT[:].rearrange("p a b -> p (a b)"), in_=bps[:, 0:8])
+        x_quant(0, 1, xg1)
+        w_quant_qk(0, 0, wg_q0)
+        ys = {}
+        ys[0] = mx_pair(0)
+        ys[1] = mx_pair(1)
+        mx_done = 2
         bS = const.tile([P, 4, 2], F32, name="bS")
         bT2 = bT[:].rearrange("p a (b c) -> p (a b) c", c=2)
         nc.vector.tensor_scalar(out=bS[:, :, 0], in0=bT2[:, :, 1], scalar1=-1.0, scalar2=None, op0=ALU.mult)
@@ -400,16 +413,7 @@ def tile_hydra_attn_pa_kernel(tc, x_bytes, x_scale, qkv_w, qkv_b, out_0, out_1, 
         nc.vector.tensor_tensor(out=rb[:], in0=cs[:, NPOS:2 * NPOS].unsqueeze(1).to_broadcast([P, 8, NPOS]),
                                 in1=bS[:].rearrange("p a b -> p (a b)").unsqueeze(2).to_broadcast([P, 8, NPOS]), op=ALU.mult)
         nc.vector.tensor_tensor(out=rb[:], in0=rb[:], in1=rb2[:], op=ALU.add)
-        x_quant(0, 1, xg1)
-        w_quant_qk(0, 0, wg_q0)
-        ys = {}
-        ys[0] = mx_pair(0)
-        ys[1] = mx_pair(1)
-        mx_done = 2
         w_quant_qk(1, 1, wg_k1)
-        bv4 = const.tile([P, 4], F32, name="bv4")
-        nc.vector.tensor_copy(out=bv4[:], in_=bv4b[:])
-        spread(bv, bv4)
         if LACE_V != 'G':
             wg_v = w_lace_v(LACE_V)
         nc.vector.quantize_mx(out=wc[2][:].bitcast(FP8X4), scales=ws[2][:], in_=wg_v[:])
@@ -438,6 +442,8 @@ def tile_hydra_attn_pa_kernel(tc, x_bytes, x_scale, qkv_w, qkv_b, out_0, out_1, 
                     trs.append((u, t4, turn_back(u, t4)))
             if s < NPAIR:
                 ps_[s], os_[s] = first_products(s, ys[s])
+            if s == 0:
+                spread_out(bv, bvp)
             for T, a2, xg in pend_quant:
                 x_quant(T, a2, xg)
                 chunk_ready[T] += 1

@@ -34,11 +34,11 @@ EV_ON_V = frozenset(((7, 1), (7, 3)))
 V_AT = {0: ((0, 0), (0, 1)), 1: ((0, 2), (0, 3)), 4: ((0, 4), (0, 5)), 5: ((0, 6), (0, 7)), 7: ((1, 0), (1, 1)), 8: ((1, 2), (1, 3)), 10: ((1, 4), (1, 5)), 11: ((1, 6), (1, 7))}
 XDEQ_AT = {0: ((1, 0),), 1: ((1, 1),), 3: ((2, 0),), 4: ((2, 1),), 6: ((3, 0),), 7: ((3, 1),)}
 MX_LEAD = 2
-V_PARTS = 4
+V_PARTS = 1
 LAG = 3
 LACE_K1 = 'A'
 LACE_K0 = 'A'
-LACE_V = 'G'
+LACE_V = 'V'
 
 
 def tile_hydra_attn_pa_kernel(tc, x_bytes, x_scale, qkv_w, qkv_b, out_0, out_1, out_2):

@@ -27,9 +27,9 @@ CHUNK = 512
 
 UNITS = [(pq, 0, ch) for ch in range(2) for pq in range(2)] + [(pq, 1, ch) for pq in range(2) for ch in range(2)]
 NPAIR = 2 * len(UNITS)
-ON_GP = ((1, 1),)
-P_B_ON_V = frozenset((11, 15))
-Y_ON_V = frozenset((8, 10, 12, 14))
+GP_UNITS = (0, 1, 3, 7)
+P_B_ON_V = frozenset((8, 10, 11, 13, 15))
+Y_ON_V = frozenset((8, 14))
 EV_ON_V = frozenset(((7, 1), (7, 3)))
 V_AT = {0: ((0, 0), (0, 1)), 1: ((0, 2), (0, 3)), 4: ((0, 4), (0, 5)), 5: ((0, 6), (0, 7)), 7: ((1, 0), (1, 1)), 8: ((1, 2), (1, 3)), 10: ((1, 4), (1, 5)), 11: ((1, 6), (1, 7))}
 XDEQ_AT = {0: ((1, 0),), 1: ((1, 1),), 3: ((2, 0),), 4: ((2, 1),), 6: ((3, 0),), 7: ((3, 1),)}
@@ -78,14 +78,10 @@ def tile_hydra_attn_pa_kernel(tc, x_bytes, x_scale, qkv_w, qkv_b, out_0, out_1, 
         load_x(0)
         for q in range(2):
             bias_q = qkv_b[q * E:(q + 1) * E]
-            for g in range(2):
-                row = brow[q * 4 + 2 * g:q * 4 + 2 * g + 2, :]
-                if (q, g) in ON_GP:
-                    nc.sync.dma_start(out=row.rearrange("p (h x) -> p h x", x=16),
-                                      in_=bias_q.rearrange("(a h x) -> a h x", a=2, x=HD)[:, :, 16 * g:16 * g + 16])
-                else:
-                    nc.sync.dma_start(out=row.rearrange("p (h i) -> p h i", i=NFREQ),
-                                      in_=bias_q.rearrange("(h f i) -> f h i", h=NH, f=4, i=NFREQ)[2 * g:2 * g + 2])
+            nc.sync.dma_start(out=brow[6 * q:6 * q + 4, :].rearrange("p (h i) -> p h i", i=NFREQ),
+                              in_=bias_q.rearrange("(h f i) -> f h i", h=NH, f=4, i=NFREQ))
+            nc.sync.dma_start(out=brow[6 * q + 4:6 * q + 6, :].rearrange("p (h x) -> p h x", x=16),
+                              in_=bias_q.rearrange("(b h x) -> b h x", b=2, x=HD)[:, :, 16:32])
         load_w(0)
         load_w(1)
         load_w(2)
@@ -98,7 +94,7 @@ def tile_hydra_attn_pa_kernel(tc, x_bytes, x_scale, qkv_w, qkv_b, out_0, out_1, 
         make_identity(nc, ident[:])
         same = const.tile([P, P], F32, name="same")
         other = const.tile([P, P], F32, name="other")
-        if ON_GP:
+        if True:
             ident_f = ident[:].rearrange("p (h f i) -> p f h i", h=8, f=2, i=NFREQ)
             nc.gpsimd.tensor_scalar(out=same[:].rearrange("p (f h i) -> p f h i", f=2, h=8), in0=ident_f, scalar1=1.0,
                                     scalar2=0.0, op0=ALU.mult, op1=ALU.add)
@@ -148,7 +144,7 @@ def tile_hydra_attn_pa_kernel(tc, x_bytes, x_scale, qkv_w, qkv_b, out_0, out_1, 
         nc.vector.tensor_reduce(out=cs[:, 0:2 * NPOS], in_=tabm[:], axis=AX.X, op=ALU.add)
         nc.vector.tensor_scalar(out=cs[:, 2 * NPOS:3 * NPOS], in0=cs[:, NPOS:2 * NPOS], scalar1=-1.0, scalar2=None,
                                 op0=ALU.mult)
-        if ON_GP:
+        if True:
             halves = const.tile([P, 2], F32, name="halves")
             nc.vector.tensor_reduce(out=halves[:], in_=ident[:].rearrange("p (h f i) -> p f h i", h=8, f=2, i=NFREQ),
                                     axis=AX.XY, op=ALU.add)
@@ -194,6 +190,13 @@ def tile_hydra_attn_pa_kernel(tc, x_bytes, x_scale, qkv_w, qkv_b, out_0, out_1, 
             ws_p = const.tile([P, E], U8, name="ws%d" % part, align_bytes=64)
             wc.append(wc_p)
             ws.append(ws_p)
+        wz = []
+        sz = []
+        for part in range(2):
+            wz_p = const.tile([P, 256], U32, name="wz%d" % part, align_bytes=64)
+            sz_p = const.tile([P, 256], U8, name="sz%d" % part, align_bytes=64)
+            wz.append(wz_p)
+            sz.append(sz_p)
 
         def lace(eng, dst, src):
             if eng == 'A':
@@ -203,12 +206,12 @@ def tile_hydra_attn_pa_kernel(tc, x_bytes, x_scale, qkv_w, qkv_b, out_0, out_1, 
             else:
                 nc.gpsimd.tensor_scalar(out=dst, in0=src, scalar1=1.0, scalar2=0.0, op0=ALU.mult, op1=ALU.add)
 
-        def w_lace_qk(part, g, eng):
+        def w_lace_qk(part, g, gp, eng):
             wg = wwork.tile([P, 2 * E], BF16, name="wgh", bufs=4, align_bytes=64)
             src = wraw[part][:].rearrange("p t (h x) -> p h x t", x=HD)
             for half in range(2):
                 dst = wg[:, half * 512:(half + 1) * 512]
-                if (part, g) in ON_GP:
+                if gp:
                     lace(eng, dst.rearrange("p (h x t) -> p h x t", h=8, x=16, t=4),
                          src[:, half * 8:(half + 1) * 8, 16 * g:16 * g + 16, :])
                 else:
@@ -216,9 +219,9 @@ def tile_hydra_attn_pa_kernel(tc, x_bytes, x_scale, qkv_w, qkv_b, out_0, out_1, 
                     lace(eng, dst.rearrange("p (h i t) -> p h i t", h=NH, i=NFREQ, t=4), src[:, :, f * 8:(f + 1) * 8, :])
             return wg
 
-        def w_quant_qk(part, g, wg):
-            nc.vector.quantize_mx(out=wc[part][:, g * 256:(g + 1) * 256].bitcast(FP8X4),
-                                  scales=ws[part][:, g * 256:(g + 1) * 256], in_=wg[:])
+        def w_quant_qk(part, g, gp, wg):
+            codes, scales = (wz[part][:], sz[part][:]) if gp else (wc[part][:, g * 256:(g + 1) * 256], ws[part][:, g * 256:(g + 1) * 256])
+            nc.vector.quantize_mx(out=codes.bitcast(FP8X4), scales=scales, in_=wg[:])
 
         def w_lace_v(eng):
             wg = wwork.tile([P, 4 * E], BF16, name="wg", bufs=1, align_bytes=64)
@@ -236,14 +239,17 @@ def tile_hydra_attn_pa_kernel(tc, x_bytes, x_scale, qkv_w, qkv_b, out_0, out_1, 
             pq, rbit, ch = UNITS[s // 2]
             return pq, rbit, ch, 1 - s % 2
 
+        def on_gp(s):
+            return s % 2 == 0 and s // 2 in GP_UNITS
+
         def mx_pair(s):
             pq, rbit, ch, g = pair_of(s)
             T = 2 * rbit + ch
             y = []
             for half in range(2):
-                f = 2 * g + half
+                codes, scales, n = (wz[pq], sz[pq], half) if on_gp(s) else (wc[pq], ws[pq], 2 * g + half)
                 y_h = psum.tile([P, 512], F32, name="y%d" % half, tag="bank")
-                mx(y_h[:], wc[pq][:, f * P:(f + 1) * P], ws[pq][:, f * P:(f + 1) * P], xc[T][:], xs[T][:])
+                mx(y_h[:], codes[:, n * P:(n + 1) * P], scales[:, n * P:(n + 1) * P], xc[T][:], xs[T][:])
                 y.append(y_h)
             return y
 
@@ -263,31 +269,21 @@ def tile_hydra_attn_pa_kernel(tc, x_bytes, x_scale, qkv_w, qkv_b, out_0, out_1, 
 
         def first_products(s, y):
             pq, rbit, ch, g = pair_of(s)
-            if (pq, g) in ON_GP:
-                yc = rot.tile([P, 2, 512], F32, name="yc%d" % g, bufs=3)
-                zc = rot.tile([P, 2, 512], F32, name="zc%d" % g, bufs=3)
+            if on_gp(s):
+                yc = rot.tile([P, 2, 512], F32, name="yc")
+                zc = rot.tile([P, 2, 512], F32, name="zc")
                 for half in range(2):
-                    bias = bT[:, pq, 2 * g + half:2 * g + half + 1]
-                    if g == 1:
-                        dst, src = yc[:, half, :], y[half][:]
-                    else:
-                        dst = yc[:, half, :].rearrange("p (w r a) -> p w r a", w=32, r=4, a=4)
-                        src = y[half][:].rearrange("p (a w r) -> p w r a", a=4, w=32, r=4)
+                    bias = bT[:, pq, 4 + half:5 + half]
                     if half == 1 and s in Y_ON_V:
-                        nc.vector.tensor_scalar(out=dst, in0=src, scalar1=bias, scalar2=None, op0=ALU.add)
+                        nc.vector.tensor_scalar(out=yc[:, half, :], in0=y[half][:], scalar1=bias, scalar2=None, op0=ALU.add)
                     else:
-                        nc.scalar.activation(out=dst, in_=src, func=ACTF.Identity, bias=bias, scale=1.0)
+                        nc.scalar.activation(out=yc[:, half, :], in_=y[half][:], func=ACTF.Identity, bias=bias, scale=1.0)
                 for k in range(4):
                     pos = position(s, k)
-                    if g == 1:
-                        yk, zk = yc[:, :, k * P:(k + 1) * P], zc[:, :, k * P:(k + 1) * P]
-                    else:
-                        yk = yc[:].rearrange("p b (w r a) -> p r b w a", w=32, r=4, a=4)[:, k]
-                        zk = zc[:].rearrange("p b (w r a) -> p r b w a", w=32, r=4, a=4)[:, k]
-                    if pos > 0 or g == 0:
+                    yk, zk = yc[:, :, k * P:(k + 1) * P], zc[:, :, k * P:(k + 1) * P]
+                    if pos > 0:
                         nc.gpsimd.tensor_scalar(out=zk, in0=yk, scalar1=cs[:, 3 * NPOS + pos:3 * NPOS + pos + 1],
                                                 scalar2=0.0, op0=ALU.mult, op1=ALU.add)
-                    if pos > 0:
                         nc.gpsimd.tensor_scalar(out=yk, in0=yk, scalar1=cs[:, pos:pos + 1], scalar2=0.0, op0=ALU.mult,
                                                 op1=ALU.add)
                 return zc, yc
@@ -314,7 +310,7 @@ def tile_hydra_attn_pa_kernel(tc, x_bytes, x_scale, qkv_w, qkv_b, out_0, out_1, 
 
         def second_products(s, y, pt, ot):
             pq, rbit, ch, g = pair_of(s)
-            if (pq, g) in ON_GP:
+            if on_gp(s):
                 return
             for half in range(2):
                 soff = 2 * NPOS if half == 0 else NPOS
@@ -343,7 +339,7 @@ def tile_hydra_attn_pa_kernel(tc, x_bytes, x_scale, qkv_w, qkv_b, out_0, out_1, 
                 cols = slice(t4 * P, (t4 + 1) * P) if g == 1 else slice(t4, 512, 4)
                 a, b = ps_[2 * u + 1 - g], os_[2 * u + 1 - g]
                 for half in range(2):
-                    if (pq, g) in ON_GP:
+                    if g == 1 and u in GP_UNITS:
                         out = tr[:, g * 256:(g + 1) * 256].rearrange("p (f b x) -> p b f x", f=2, b=2)[:, half]
                         one = g == 1 and position(2 * u, t4) == 0
                         nc.tensor.matmul(out=out, lhsT=b[:, half, cols], rhs=same[:], is_transpose=True, start=True, stop=one)
@@ -375,11 +371,14 @@ def tile_hydra_attn_pa_kernel(tc, x_bytes, x_scale, qkv_w, qkv_b, out_0, out_1, 
             nc.vector.tensor_tensor(out=out_t[2][:, :, rbit, c, :], in0=yv_[:].rearrange("p (h d) -> p h d", d=HD),
                                     in1=bv[:].rearrange("p (h d) -> p h d", d=HD), op=ALU.add)
 
-        wg_q1 = w_lace_qk(0, 1, 'G')
-        wg_q0 = w_lace_qk(0, 0, 'A')
-        if LACE_V == 'G':
-            wg_v = w_lace_v('G')
-        wg_k1 = w_lace_qk(1, 1, LACE_K1)
+        gp_q, gp_k = 0 in GP_UNITS, 1 in GP_UNITS
+        more_q = any(UNITS[u][0] == 0 and (u in GP_UNITS) != gp_q for u in range(len(UNITS)))
+        more_k = any(UNITS[u][0] == 1 and (u in GP_UNITS) != gp_k for u in range(len(UNITS)))
+        wg_q1 = w_lace_qk(0, 1, gp_q, 'G')
+        if more_q:
+            wg_q1b = w_lace_qk(0, 1, not gp_q, 'G')
+        wg_q0 = w_lace_qk(0, 0, False, 'A')
+        wg_k1 = w_lace_qk(1, 1, gp_k, LACE_K1)
         browf = const.tile([P, P], F32, name="browf")
         nc.vector.tensor_copy(out=browf[:], in_=brow[:])
         bps = psum.tile([P, 512], F32, name="bps", tag="bank")
@@ -388,36 +387,37 @@ def tile_hydra_attn_pa_kernel(tc, x_bytes, x_scale, qkv_w, qkv_b, out_0, out_1, 
         xt1 = x_widen(0, 1)
         xg0 = x_copy(xt0)
         xg1 = x_copy(xt1)
-        wg_k0 = w_lace_qk(1, 0, LACE_K0)
+        wg_k0 = w_lace_qk(1, 0, False, LACE_K0)
         bv4 = const.tile([P, 4], F32, name="bv4")
         nc.vector.tensor_copy(out=bv4[:], in_=bv4b[:])
         bvp = spread(bv4)
         x_quant(0, 0, xg0)
-        w_quant_qk(0, 1, wg_q1)
-        bT = const.tile([P, 2, 4], F32, name="bT")
-        nc.vector.tensor_copy(out=bT[:].rearrange("p a b -> p (a b)"), in_=bps[:, 0:8])
+        w_quant_qk(0, 1, gp_q, wg_q1)
+        bT = const.tile([P, 2, 6], F32, name="bT")
+        nc.vector.tensor_copy(out=bT[:].rearrange("p a b -> p (a b)"), in_=bps[:, 0:12])
         x_quant(0, 1, xg1)
-        w_quant_qk(0, 0, wg_q0)
+        w_quant_qk(0, 0, False, wg_q0)
         ys = {}
         ys[0] = mx_pair(0)
         ys[1] = mx_pair(1)
         mx_done = 2
         bS = const.tile([P, 4, 2], F32, name="bS")
-        bT2 = bT[:].rearrange("p a (b c) -> p (a b) c", c=2)
+        bR = const.tile([P, 2, 4], F32, name="bR")
+        nc.vector.tensor_copy(out=bR[:], in_=bT[:, :, 0:4])
+        bT2 = bR[:].rearrange("p a (b c) -> p (a b) c", c=2)
         nc.vector.tensor_scalar(out=bS[:, :, 0], in0=bT2[:, :, 1], scalar1=-1.0, scalar2=None, op0=ALU.mult)
         nc.vector.tensor_copy(out=bS[:, :, 1], in_=bT2[:, :, 0])
         rb = const.tile([P, 8, NPOS], F32, name="rb")
         rb2 = const.tile([P, 8, NPOS], F32, name="rb2")
         nc.vector.tensor_tensor(out=rb2[:], in0=cs[:, 0:NPOS].unsqueeze(1).to_broadcast([P, 8, NPOS]),
-                                in1=bT[:].rearrange("p a b -> p (a b)").unsqueeze(2).to_broadcast([P, 8, NPOS]), op=ALU.mult)
+                                in1=bR[:].rearrange("p a b -> p (a b)").unsqueeze(2).to_broadcast([P, 8, NPOS]), op=ALU.mult)
         nc.vector.tensor_tensor(out=rb[:], in0=cs[:, NPOS:2 * NPOS].unsqueeze(1).to_broadcast([P, 8, NPOS]),
                                 in1=bS[:].rearrange("p a b -> p (a b)").unsqueeze(2).to_broadcast([P, 8, NPOS]), op=ALU.mult)
         nc.vector.tensor_tensor(out=rb[:], in0=rb[:], in1=rb2[:], op=ALU.add)
-        w_quant_qk(1, 1, wg_k1)
-        if LACE_V != 'G':
-            wg_v = w_lace_v(LACE_V)
+        w_quant_qk(1, 1, gp_k, wg_k1)
+        wg_v = w_lace_v(LACE_V)
         nc.vector.quantize_mx(out=wc[2][:].bitcast(FP8X4), scales=ws[2][:], in_=wg_v[:])
-        w_quant_qk(1, 0, wg_k0)
+        w_quant_qk(1, 0, False, wg_k0)
         pend_copy = []
         pend_quant = []
         chunk_ready = {0: 2, 1: 0, 2: 0, 3: 0}
@@ -435,6 +435,12 @@ def tile_hydra_attn_pa_kernel(tc, x_bytes, x_scale, qkv_w, qkv_b, out_0, out_1, 
                 if v_count[rbit] == NPOS:
                     store(2, rbit)
             pend_v = []
+            if s == 1 and more_q:
+                w_quant_qk(0, 1, not gp_q, wg_q1b)
+            if s == 3 and more_k:
+                wg_k1b = w_lace_qk(1, 1, not gp_k, 'G')
+            if s == 6 and more_k:
+                w_quant_qk(1, 1, not gp_k, wg_k1b)
             trs = []
             if s >= LAG:
                 u = (s - LAG) // 2

import math
from contextlib import ExitStack

import concourse.mybir as mybir
from concourse.masks import make_identity

FLOPS = 2 * 2048 * 512 * 1536

F32 = mybir.dt.float32
BF16 = mybir.dt.bfloat16
U32 = mybir.dt.uint32
U8 = mybir.dt.uint8
FP8 = mybir.dt.float8_e4m3fn
FP8X4 = mybir.dt.float8_e4m3fn_x4
ALU = mybir.AluOpType
ACTF = mybir.ActivationFunctionType
AX = mybir.AxisListType

P = 128
NPOS = 8
NFREQ = 8
NH = 16
HD = 32
E = 512
KDIM = 512
CHUNK = 512

UNITS = [(pq, 0, ch) for ch in range(2) for pq in range(2)] + [(pq, 1, ch) for pq in range(2) for ch in range(2)]
NPAIR = 2 * len(UNITS)
GP_UNITS = (0, 1, 3, 7)
P_B_ON_V = frozenset((8, 10, 11, 13, 15))
Y_ON_V = frozenset((8, 14))
EV_ON_V = frozenset(((7, 1), (7, 3)))
V_AT = {0: ((0, 0), (0, 1)), 1: ((0, 2), (0, 3)), 4: ((0, 4), (0, 5)), 5: ((0, 6), (0, 7)), 7: ((1, 0), (1, 1)), 8: ((1, 2), (1, 3)), 10: ((1, 4), (1, 5)), 11: ((1, 6), (1, 7))}
XDEQ_AT = {0: ((1, 0),), 1: ((1, 1),), 3: ((2, 0),), 4: ((2, 1),), 6: ((3, 0),), 7: ((3, 1),)}
MX_LEAD = 2
V_PARTS = 1
LAG = 3
LACE_K1 = 'A'
LACE_K0 = 'A'
LACE_V = 'V'


def tile_hydra_attn_pa_kernel(tc, x_bytes, x_scale, qkv_w, qkv_b, out_0, out_1, out_2):
    nc = tc.nc
    outs = (out_0, out_1, out_2)

    with ExitStack() as ctx:
        const = ctx.enter_context(tc.tile_pool(name="const", bufs=1))
        xwork = ctx.enter_context(tc.tile_pool(name="xwork", bufs=3))
        wwork = ctx.enter_context(tc.tile_pool(name="wwork", bufs=2))
        rot = ctx.enter_context(tc.tile_pool(name="rot", bufs=3))
        psum = ctx.enter_context(tc.psum_pool(name="psum", bufs=8))
        ctx.enter_context(tc.manual_schedule())

        x_rows = x_bytes.rearrange("b (wi rp rb) (j c) k -> rb (b wi rp) j (c k)", wi=2, rp=4, rb=2, j=2)
        w_rows = qkv_w.rearrange("(p t) n -> p t n", t=4)
        xb = []
        wraw = []
        for T in range(4):
            xb_T = const.tile([P, 4 * KDIM], U8, name="xb%d" % T)
            xb.append(xb_T)
        for part in range(3):
            wraw_p = const.tile([P, 4, E], BF16, name="wraw%d" % part)
            wraw.append(wraw_p)

        def load_x(T):
            nc.sync.dma_start(out=xb[T][:], in_=x_rows[T // 2, :, :, (T % 2) * 2048:(T % 2 + 1) * 2048])

        def load_w(part):
            nc.sync.dma_start(out=wraw[part][:], in_=w_rows[:, :, part * E:(part + 1) * E])

        brow = const.tile([P, P], BF16, name="brow")
        nc.vector.memset(brow[:], 0.0)
        sc4 = const.tile([P, 4], F32, name="sc4")
        bv4b = const.tile([P, 4], BF16, name="bv4b")
        nc.sync.dma_start(out=sc4[:], in_=x_scale.rearrange("a b c (p g) -> p (a b c g)", p=P, g=4))
        load_x(0)
        for q in range(2):
            bias_q = qkv_b[q * E:(q + 1) * E]
            nc.sync.dma_start(out=brow[6 * q:6 * q + 4, :].rearrange("p (h i) -> p h i", i=NFREQ),
                              in_=bias_q.rearrange("(h f i) -> f h i", h=NH, f=4, i=NFREQ))
            nc.sync.dma_start(out=brow[6 * q + 4:6 * q + 6, :].rearrange("p (h x) -> p h x", x=16),
                              in_=bias_q.rearrange("(b h x) -> b h x", b=2, x=HD)[:, :, 16:32])
        load_w(0)
        load_w(1)
        load_w(2)
        nc.sync.dma_start(out=bv4b[:], in_=qkv_b[2 * E:3 * E].rearrange("(p g) -> p g", p=P, g=4))
        load_x(1)
        load_x(2)
        load_x(3)

        ident = const.tile([P, P], F32, name="ident")
        make_identity(nc, ident[:])
        same = const.tile([P, P], F32, name="same")
        other = const.tile([P, P], F32, name="other")
        if True:
            ident_f = ident[:].rearrange("p (h f i) -> p f h i", h=8, f=2, i=NFREQ)
            nc.gpsimd.tensor_scalar(out=same[:].rearrange("p (f h i) -> p f h i", f=2, h=8), in0=ident_f, scalar1=1.0,
                                    scalar2=0.0, op0=ALU.mult, op1=ALU.add)
            for f in range(2):
                nc.gpsimd.tensor_scalar(out=other[:, f * 64:(f + 1) * 64].rearrange("p (h i) -> p h i", h=8),
                                        in0=ident_f[:, 1 - f], scalar1=1.0, scalar2=0.0, op0=ALU.mult, op1=ALU.add)
        sc = const.tile([P, KDIM], F32, name="sc")
        bv = const.tile([P, E], F32, name="bv")

        def spread(v4):
            sp = psum.tile([P, 512], F32, name="sp", tag="bank")
            for g in range(4):
                nc.tensor.transpose(sp[:, g * P:(g + 1) * P], v4[:, g:g + 1].to_broadcast([P, P]), ident[:])
            return sp

        def spread_out(dst, sp):
            nc.scalar.copy(out=dst[:].rearrange("p (n g) -> p n g", g=4), in_=sp[:].rearrange("p (g n) -> p n g", g=4))

        zo = const.tile([P, 2], F32, name="zo")
        nc.vector.memset(zo[:, 0:1], 0.0)
        nc.vector.memset(zo[:, 1:2], 1.0)
        tab = const.tile([P, 2, NPOS, NFREQ], F32, name="tab")
        nc.vector.memset(tab[:, 0, 0, :], 1.0)
        nc.vector.memset(tab[:, 1, 0, :], 0.0)
        for pos in range(1, NPOS):
            for s in range(2):
                for i in range(0, NFREQ, 2):
                    ang = (pos * 10000.0 ** (-i / 8.0), pos * 10000.0 ** (-(i + 1) / 8.0))
                    va = math.cos(ang[0]) if s == 0 else math.sin(ang[0])
                    vb = math.cos(ang[1]) if s == 0 else math.sin(ang[1])
                    dst = tab[:, s, pos, i:i + 2]
                    if s == 0:
                        nc.vector.tensor_scalar(out=dst, in0=zo[:], scalar1=vb - va, scalar2=va, op0=ALU.mult,
                                                op1=ALU.add)
                    else:
                        nc.scalar.activation(out=dst, in_=zo[:], func=ACTF.Copy, bias=va, scale=vb - va)
        spread_out(sc, spread(sc4))
        perm = const.tile([P, P], F32, name="perm")
        nc.vector.tensor_copy(out=perm[:].rearrange("p (b j r) -> p b j r", b=16, j=2, r=4),
                              in_=ident[:].rearrange("p (b r j) -> p b j r", b=16, r=4, j=2))
        pick = const.tile([P, NFREQ], F32, name="pick")
        nc.vector.tensor_reduce(out=pick[:], in_=ident[:].rearrange("p (h i) -> p i h", i=NFREQ), axis=AX.X, op=ALU.add)
        tabm = const.tile([P, 2 * NPOS, NFREQ], F32, name="tabm")
        nc.vector.tensor_tensor(out=tabm[:], in0=tab[:].rearrange("p s q i -> p (s q) i"),
                                in1=pick[:].unsqueeze(1).to_broadcast([P, 2 * NPOS, NFREQ]), op=ALU.mult)
        cs = const.tile([P, 4 * NPOS], F32, name="cs")
        nc.vector.tensor_reduce(out=cs[:, 0:2 * NPOS], in_=tabm[:], axis=AX.X, op=ALU.add)
        nc.vector.tensor_scalar(out=cs[:, 2 * NPOS:3 * NPOS], in0=cs[:, NPOS:2 * NPOS], scalar1=-1.0, scalar2=None,
                                op0=ALU.mult)
        if True:
            halves = const.tile([P, 2], F32, name="halves")
            nc.vector.tensor_reduce(out=halves[:], in_=ident[:].rearrange("p (h f i) -> p f h i", h=8, f=2, i=NFREQ),
                                    axis=AX.XY, op=ALU.add)
            sign = const.tile([P, 1], F32, name="sign")
            nc.vector.tensor_tensor(out=sign[:], in0=halves[:, 0:1], in1=halves[:, 1:2], op=ALU.subtract)
            nc.vector.tensor_scalar(out=cs[:, 3 * NPOS:4 * NPOS], in0=cs[:, NPOS:2 * NPOS], scalar1=sign[:], scalar2=None,
                                    op0=ALU.mult)

        xc = []
        xs = []
        for T in range(4):
            xc_T = const.tile([P, CHUNK], U32, name="xc%d" % T, align_bytes=64)
            xs_T = const.tile([P, CHUNK], U8, name="xs%d" % T, align_bytes=64)
            xc.append(xc_T)
            xs.append(xs_T)

        def x_widen(T, a2):
            xt = psum.tile([P, 512], F32, name="xt", tag="bank")
            for a in range(2):
                t4 = 2 * a2 + a
                xq = xwork.tile([P, KDIM], BF16, name="xq", bufs=4)
                nc.vector.tensor_tensor(out=xq[:], in0=xb[T][:, t4 * KDIM:(t4 + 1) * KDIM].bitcast(FP8),
                                        in1=sc[:], op=ALU.mult)
                words = xq[:].bitcast(F32)
                for u in range(2):
                    nc.tensor.transpose(xt[:, (2 * a + u) * P:(2 * a + u + 1) * P], words[:, u:256:2], perm[:])
            return xt

        def x_copy(xt):
            xg = xwork.tile([P, 1024], BF16, name="xg", align_bytes=64)
            nc.scalar.copy(out=xg[:].bitcast(F32).rearrange("p (a m u) -> p a m u", a=2, u=2),
                           in_=xt[:].rearrange("p (a u m) -> p a m u", a=2, u=2))
            return xg

        def x_quant(T, a2, xg):
            nc.vector.quantize_mx(out=xc[T][:, a2 * 256:(a2 + 1) * 256].bitcast(FP8X4),
                                  scales=xs[T][:, a2 * 256:(a2 + 1) * 256], in_=xg[:])

        wc = []
        ws = []
        for part in range(3):
            wc_p = const.tile([P, E], U32, name="wc%d" % part, align_bytes=64)
            ws_p = const.tile([P, E], U8, name="ws%d" % part, align_bytes=64)
            wc.append(wc_p)
            ws.append(ws_p)
        wz = []
        sz = []
        for part in range(2):
            wz_p = const.tile([P, 256], U32, name="wz%d" % part, align_bytes=64)
            sz_p = const.tile([P, 256], U8, name="sz%d" % part, align_bytes=64)
            wz.append(wz_p)
            sz.append(sz_p)

        def lace(eng, dst, src):
            if eng == 'A':
                nc.scalar.copy(out=dst, in_=src)
            elif eng == 'V':
                nc.vector.tensor_copy(out=dst, in_=src)
            else:
                nc.gpsimd.tensor_scalar(out=dst, in0=src, scalar1=1.0, scalar2=0.0, op0=ALU.mult, op1=ALU.add)

        def w_lace_qk(part, g, gp, eng):
            wg = wwork.tile([P, 2 * E], BF16, name="wgh", bufs=4, align_bytes=64)
            src = wraw[part][:].rearrange("p t (h x) -> p h x t", x=HD)
            for half in range(2):
                dst = wg[:, half * 512:(half + 1) * 512]
                if gp:
                    lace(eng, dst.rearrange("p (h x t) -> p h x t", h=8, x=16, t=4),
                         src[:, half * 8:(half + 1) * 8, 16 * g:16 * g + 16, :])
                else:
                    f = 2 * g + half
                    lace(eng, dst.rearrange("p (h i t) -> p h i t", h=NH, i=NFREQ, t=4), src[:, :, f * 8:(f + 1) * 8, :])
            return wg

        def w_quant_qk(part, g, gp, wg):
            codes, scales = (wz[part][:], sz[part][:]) if gp else (wc[part][:, g * 256:(g + 1) * 256], ws[part][:, g * 256:(g + 1) * 256])
            nc.vector.quantize_mx(out=codes.bitcast(FP8X4), scales=scales, in_=wg[:])

        def w_lace_v(eng):
            wg = wwork.tile([P, 4 * E], BF16, name="wg", bufs=1, align_bytes=64)
            n = E // V_PARTS
            for c in range(V_PARTS):
                lace(eng, wg[:, c * 4 * n:(c + 1) * 4 * n].rearrange("p (n t) -> p n t", t=4),
                     wraw[2][:, :, c * n:(c + 1) * n].rearrange("p t n -> p n t"))
            return wg

        def mx(out, lc, ls, rc, rs):
            nc.tensor.matmul_mx(out=out, lhsT=lc.bitcast(FP8X4), lhsT_scale=ls, rhs=rc.bitcast(FP8X4), rhs_scale=rs,
                                start=True, stop=True)

        def pair_of(s):
            pq, rbit, ch = UNITS[s // 2]
            return pq, rbit, ch, 1 - s % 2

        def on_gp(s):
            return s % 2 == 0 and s // 2 in GP_UNITS

        def mx_pair(s):
            pq, rbit, ch, g = pair_of(s)
            T = 2 * rbit + ch
            y = []
            for half in range(2):
                codes, scales, n = (wz[pq], sz[pq], half) if on_gp(s) else (wc[pq], ws[pq], 2 * g + half)
                y_h = psum.tile([P, 512], F32, name="y%d" % half, tag="bank")
                mx(y_h[:], codes[:, n * P:(n + 1) * P], scales[:, n * P:(n + 1) * P], xc[T][:], xs[T][:])
                y.append(y_h)
            return y

        def psum_view(t, g, k):
            if g == 1:
                return t[:, k * P:(k + 1) * P]
            return t[:].rearrange("p (a w r) -> p r w a", a=4, w=32, r=4)[:, k]

        def sbuf_view(t, g, k):
            if g == 1:
                return t[:, k * P:(k + 1) * P]
            return t[:].rearrange("p (w r a) -> p r w a", w=32, r=4, a=4)[:, k]

        def position(s, k):
            pq, rbit, ch, g = pair_of(s)
            return 4 * ch + k if g == 1 else 2 * k + rbit

        def first_products(s, y):
            pq, rbit, ch, g = pair_of(s)
            if on_gp(s):
                yc = rot.tile([P, 2, 512], F32, name="yc")
                zc = rot.tile([P, 2, 512], F32, name="zc")
                for half in range(2):
                    bias = bT[:, pq, 4 + half:5 + half]
                    if half == 1 and s in Y_ON_V:
                        nc.vector.tensor_scalar(out=yc[:, half, :], in0=y[half][:], scalar1=bias, scalar2=None, op0=ALU.add)
                    else:
                        nc.scalar.activation(out=yc[:, half, :], in_=y[half][:], func=ACTF.Identity, bias=bias, scale=1.0)
                for k in range(4):
                    pos = position(s, k)
                    yk, zk = yc[:, :, k * P:(k + 1) * P], zc[:, :, k * P:(k + 1) * P]
                    if pos > 0:
                        nc.gpsimd.tensor_scalar(out=zk, in0=yk, scalar1=cs[:, 3 * NPOS + pos:3 * NPOS + pos + 1],
                                                scalar2=0.0, op0=ALU.mult, op1=ALU.add)
                        nc.gpsimd.tensor_scalar(out=yk, in0=yk, scalar1=cs[:, pos:pos + 1], scalar2=0.0, op0=ALU.mult,
                                                op1=ALU.add)
                return zc, yc
            pt = []
            ot = []
            for half in range(2):
                p_h = rot.tile([P, 512], F32, name="p%d%d" % (g, half))
                o_h = rot.tile([P, 512], F32, name="o%d%d" % (g, half))
                pt.append(p_h)
                ot.append(o_h)
            for half in range(2):
                col = pq * 4 + 2 * g + half
                for k in range(4):
                    pos = position(s, k)
                    dst = sbuf_view(ot[half] if pos == 0 else pt[half], g, k)
                    src = psum_view(y[half], g, k)
                    if half == 1 and s in P_B_ON_V:
                        nc.vector.tensor_scalar(out=dst, in0=src, scalar1=cs[:, pos:pos + 1],
                                                scalar2=rb[:, col, pos:pos + 1], op0=ALU.mult, op1=ALU.add)
                    else:
                        nc.scalar.activation(out=dst, in_=src, func=ACTF.Identity, bias=rb[:, col, pos:pos + 1],
                                             scale=cs[:, pos:pos + 1])
            return pt, ot

        def second_products(s, y, pt, ot):
            pq, rbit, ch, g = pair_of(s)
            if on_gp(s):
                return
            for half in range(2):
                soff = 2 * NPOS if half == 0 else NPOS
                for k in range(4):
                    pos = position(s, k)
                    if pos > 0:
                        nc.vector.scalar_tensor_tensor(out=sbuf_view(ot[half], g, k), in0=psum_view(y[1 - half], g, k),
                                                       scalar=cs[:, soff + pos:soff + pos + 1],
                                                       in1=sbuf_view(pt[half], g, k), op0=ALU.mult, op1=ALU.add)

        out_t = []
        for part in range(3):
            out_p = const.tile([P, NH, 2, NPOS, HD], F32, name="out%d" % part)
            out_t.append(out_p)

        def store(part, rbit):
            dst = outs[part].rearrange("w h (rp rb c) d -> rp rb w h c d", rp=4, rb=2, c=8)
            for rp in range(4):
                nc.sync.dma_start(out=dst[rp, rbit].rearrange("w h c d -> w h (c d)"),
                                  in_=out_t[part][rp:P:4, :, rbit].rearrange("p h c d -> p h (c d)"))

        def turn_back(u, t4):
            pq, rbit, ch = UNITS[u]
            tr = psum.tile([P, 512], F32, name="tr", tag="bank")
            for g in range(2):
                cols = slice(t4 * P, (t4 + 1) * P) if g == 1 else slice(t4, 512, 4)
                a, b = ps_[2 * u + 1 - g], os_[2 * u + 1 - g]
                for half in range(2):
                    if g == 1 and u in GP_UNITS:
                        out = tr[:, g * 256:(g + 1) * 256].rearrange("p (f b x) -> p b f x", f=2, b=2)[:, half]
                        one = g == 1 and position(2 * u, t4) == 0
                        nc.tensor.matmul(out=out, lhsT=b[:, half, cols], rhs=same[:], is_transpose=True, start=True, stop=one)
                        if not one:
                            nc.tensor.matmul(out=out, lhsT=a[:, half, cols], rhs=other[:], is_transpose=True, start=False,
                                             stop=True)
                    else:
                        f = 2 * g + half
                        nc.tensor.transpose(tr[:, f * P:(f + 1) * P], b[half][:, cols], ident[:])
            return tr

        def copy_out(tr, u, t4):
            pq, rbit, ch = UNITS[u]
            dst = out_t[pq][:, :, rbit, 4 * ch + t4, :].rearrange("p h (f i) -> p h f i", f=4)
            src = tr[:].rearrange("p (f h i) -> p h f i", f=4, h=NH, i=NFREQ)
            if (u, t4) in EV_ON_V:
                nc.vector.tensor_copy(out=dst, in_=src)
            else:
                nc.scalar.copy(out=dst, in_=src)

        def v_mx(rbit, c):
            T = 2 * rbit + c // 4
            t4 = c % 4
            yv_ = psum.tile([P, 512], F32, name="yv_", tag="bank")
            mx(yv_[:], xc[T][:, t4 * P:(t4 + 1) * P], xs[T][:, t4 * P:(t4 + 1) * P], wc[2][:], ws[2][:])
            return yv_

        def v_add(yv_, rbit, c):
            nc.vector.tensor_tensor(out=out_t[2][:, :, rbit, c, :], in0=yv_[:].rearrange("p (h d) -> p h d", d=HD),
                                    in1=bv[:].rearrange("p (h d) -> p h d", d=HD), op=ALU.add)

        gp_q, gp_k = 0 in GP_UNITS, 1 in GP_UNITS
        more_q = any(UNITS[u][0] == 0 and (u in GP_UNITS) != gp_q for u in range(len(UNITS)))
        more_k = any(UNITS[u][0] == 1 and (u in GP_UNITS) != gp_k for u in range(len(UNITS)))
        wg_q1 = w_lace_qk(0, 1, gp_q, 'G')
        if more_q:
            wg_q1b = w_lace_qk(0, 1, not gp_q, 'G')
        wg_q0 = w_lace_qk(0, 0, False, 'A')
        wg_k1 = w_lace_qk(1, 1, gp_k, LACE_K1)
        browf = const.tile([P, P], F32, name="browf")
        nc.vector.tensor_copy(out=browf[:], in_=brow[:])
        bps = psum.tile([P, 512], F32, name="bps", tag="bank")
        nc.tensor.transpose(bps[:, 0:P], browf[:], ident[:])
        xt0 = x_widen(0, 0)
        xt1 = x_widen(0, 1)
        xg0 = x_copy(xt0)
        xg1 = x_copy(xt1)
        wg_k0 = w_lace_qk(1, 0, False, LACE_K0)
        bv4 = const.tile([P, 4], F32, name="bv4")
        nc.vector.tensor_copy(out=bv4[:], in_=bv4b[:])
        bvp = spread(bv4)
        x_quant(0, 0, xg0)
        w_quant_qk(0, 1, gp_q, wg_q1)
        bT = const.tile([P, 2, 6], F32, name="bT")
        nc.vector.tensor_copy(out=bT[:].rearrange("p a b -> p (a b)"), in_=bps[:, 0:12])
        x_quant(0, 1, xg1)
        w_quant_qk(0, 0, False, wg_q0)
        ys = {}
        ys[0] = mx_pair(0)
        ys[1] = mx_pair(1)
        mx_done = 2
        bS = const.tile([P, 4, 2], F32, name="bS")
        bR = const.tile([P, 2, 4], F32, name="bR")
        nc.vector.tensor_copy(out=bR[:], in_=bT[:, :, 0:4])
        bT2 = bR[:].rearrange("p a (b c) -> p (a b) c", c=2)
        nc.vector.tensor_scalar(out=bS[:, :, 0], in0=bT2[:, :, 1], scalar1=-1.0, scalar2=None, op0=ALU.mult)
        nc.vector.tensor_copy(out=bS[:, :, 1], in_=bT2[:, :, 0])
        rb = const.tile([P, 8, NPOS], F32, name="rb")
        rb2 = const.tile([P, 8, NPOS], F32, name="rb2")
        nc.vector.tensor_tensor(out=rb2[:], in0=cs[:, 0:NPOS].unsqueeze(1).to_broadcast([P, 8, NPOS]),
                                in1=bR[:].rearrange("p a b -> p (a b)").unsqueeze(2).to_broadcast([P, 8, NPOS]), op=ALU.mult)
        nc.vector.tensor_tensor(out=rb[:], in0=cs[:, NPOS:2 * NPOS].unsqueeze(1).to_broadcast([P, 8, NPOS]),
                                in1=bS[:].rearrange("p a b -> p (a b)").unsqueeze(2).to_broadcast([P, 8, NPOS]), op=ALU.mult)
        nc.vector.tensor_tensor(out=rb[:], in0=rb[:], in1=rb2[:], op=ALU.add)
        w_quant_qk(1, 1, gp_k, wg_k1)
        wg_v = w_lace_v(LACE_V)
        nc.vector.quantize_mx(out=wc[2][:].bitcast(FP8X4), scales=ws[2][:], in_=wg_v[:])
        w_quant_qk(1, 0, False, wg_k0)
        pend_copy = []
        pend_quant = []
        chunk_ready = {0: 2, 1: 0, 2: 0, 3: 0}
        pend_v = []
        v_count = {0: 0, 1: 0}
        ps_ = {}
        os_ = {}

        for s in range(NPAIR + LAG):
            if 1 <= s <= NPAIR:
                second_products(s - 1, ys[s - 1], ps_[s - 1], os_[s - 1])
            for rbit, c, yv_ in pend_v:
                v_add(yv_, rbit, c)
                v_count[rbit] += 1
                if v_count[rbit] == NPOS:
                    store(2, rbit)
            pend_v = []
            if s == 1 and more_q:
                w_quant_qk(0, 1, not gp_q, wg_q1b)
            if s == 3 and more_k:
                wg_k1b = w_lace_qk(1, 1, not gp_k, 'G')
            if s == 6 and more_k:
                w_quant_qk(1, 1, not gp_k, wg_k1b)
            trs = []
            if s >= LAG:
                u = (s - LAG) // 2
                for t4 in ((0, 1) if (s - LAG) % 2 == 0 else (2, 3)):
                    trs.append((u, t4, turn_back(u, t4)))
            if s < NPAIR:
                ps_[s], os_[s] = first_products(s, ys[s])
            if s == 0:
                spread_out(bv, bvp)
            for T, a2, xg in pend_quant:
                x_quant(T, a2, xg)
                chunk_ready[T] += 1
            pend_quant = []
            while mx_done < NPAIR and mx_done <= s + MX_LEAD:
                npq, nrb, nch, ng = pair_of(mx_done)
                if chunk_ready[2 * nrb + nch] < 2:
                    break
                ys[mx_done] = mx_pair(mx_done)
                mx_done += 1
            for rbit, c in V_AT.get(s, ()):
                pend_v.append((rbit, c, v_mx(rbit, c)))
            for u, t4, tr in trs:
                copy_out(tr, u, t4)
            for T, a2, xt in pend_copy:
                pend_quant.append((T, a2, x_copy(xt)))
            pend_copy = []
            for T, a2 in XDEQ_AT.get(s, ()):
                pend_copy.append((T, a2, x_widen(T, a2)))
            if s > LAG and (s - LAG) % 2 == 1:
                u = (s - LAG) // 2
                if UNITS[u][2] == 1:
                    store(UNITS[u][0], UNITS[u][1])
